import numpy as np
import ml_dtypes


def mxq(x, axis, fmt="e4m3"):
    dtype, down = {"e4m3": (ml_dtypes.float8_e4m3fn, 7), "e5m2": (ml_dtypes.float8_e5m2, 14)}[fmt]
    v = np.moveaxis(np.asarray(x, np.float32).astype(ml_dtypes.bfloat16).astype(np.float64), axis, -1)
    blocks = v.reshape(v.shape[:-1] + (-1, 32))
    amax = np.abs(blocks).max(-1, keepdims=True)
    byte = np.maximum(np.where(amax > 0, np.frexp(amax)[1] - 1 + 127, 0) - down, 1)
    scale = np.exp2(byte - 127.0)
    codes = (blocks / scale).astype(np.float32).astype(dtype).astype(np.float64)
    return np.moveaxis((codes * scale).reshape(v.shape), -1, axis)


WIDE = False


def mx_kscale(k):
    if not WIDE:
        return np.ones(k)
    levels = np.array([10, -10, 5, -5, 0])
    a = np.random.permutation(np.resize(levels, k // 512 * 4)).reshape(k // 512, 4)
    idx = np.arange(k)
    return np.exp2(a[idx // 512, idx % 128 // 32])


BF16 = ml_dtypes.bfloat16


def bf(x):
    return np.asarray(x, np.float32).astype(BF16)


def f64(x):
    return np.asarray(x).astype(np.float64)


B, S, FIN, D, AF, F, H = 2, 256, 128, 1024, 2048, 4096, 16
EPS = 1e-3


def layer_norm(v, gamma, beta):
    mu = v.mean(-1, keepdims=True)
    var = v.var(-1, keepdims=True)
    return (v - mu) / np.sqrt(var + EPS) * gamma + beta


def setup_inputs():
    r = np.random.standard_normal
    t = mx_kscale(F)
    return {"h_attn": bf(r((B, S, D))),
            "W1": bf(r((D, F)) / np.sqrt(D) * t), "b1": bf(0.1 * r(F) * t),
            "W2": bf(r((F, D)) / np.sqrt(F) / t[:, None]), "b2": bf(0.1 * r(D)),
            "g2": bf(1.0 + 0.1 * r(D)), "beta2": bf(0.1 * r(D))}


def reference(h_attn, W1, b1, W2, b2, g2, beta2):
    h = f64(h_attn)
    hid = np.maximum((mxq(h, 2, "e4m3") @ mxq(f64(W1), 0, "e4m3")) + f64(b1), 0.0)
    ffn = (mxq(hid, 2, "e4m3") @ mxq(f64(W2), 0, "e4m3")) + f64(b2)
    return layer_norm(h + ffn, f64(g2), f64(beta2))

@@ -1,0 +1,245 @@
+from contextlib import ExitStack
+
+import concourse.mybir as mybir
+from concourse.masks import make_identity
+
+F32 = mybir.dt.float32
+BF16 = mybir.dt.bfloat16
+U32 = mybir.dt.uint32
+U8 = mybir.dt.uint8
+FP8X4 = mybir.dt.float8_e4m3fn_x4
+ACT = mybir.ActivationFunctionType
+ALU = mybir.AluOpType
+
+P = 128
+PACK = 4
+K_PASS = P * PACK
+TOK = 512
+D = 1024
+F = 4096
+EPS = 1e-3
+N_TILE = 512
+TOK_TILES = TOK // P
+D_PASSES = D // K_PASS
+F_BLOCKS = F // K_PASS
+D_HALVES = D // N_TILE
+AHEAD = 8
+
+FLOPS = 2 * TOK * D * F * 2
+
+
+def regroup(engine_copy, grouped, rows):
+    engine_copy(
+        out=grouped.rearrange("p (c i) j -> p c j i", i=4),
+        in_=rows.rearrange("p j (c i) -> p c j i", i=4),
+    )
+
+
+def tile_ffnn_encoder_pc_kernel(tc, h_attn, W1, b1, W2, b2, g2, beta2, out):
+    nc = tc.nc
+    h_rows = h_attn.rearrange("b s d -> (b s) d")
+    out_rows = out.rearrange("b s d -> (b s) d")
+
+    with ExitStack() as ctx:
+        keep = ctx.enter_context(tc.tile_pool(name="keep", bufs=1))
+        raw_pool = ctx.enter_context(tc.tile_pool(name="raw", bufs=AHEAD + 1))
+        grouped_pool = ctx.enter_context(tc.tile_pool(name="grouped", bufs=4))
+        codes_pool = ctx.enter_context(tc.tile_pool(name="codes", bufs=6))
+        hid_pool = ctx.enter_context(tc.tile_pool(name="hid", bufs=3))
+        norm_pool = ctx.enter_context(tc.tile_pool(name="norm", bufs=4))
+        psum = ctx.enter_context(tc.psum_pool(name="psum", bufs=8))
+
+        eps_col = keep.tile([P, 1], F32)
+        nc.vector.memset(eps_col[:], EPS)
+        warm_col = keep.tile([P, 1], F32)
+        nc.scalar.activation(out=warm_col[:], in_=eps_col[:], func=ACT.Sqrt)
+        ident_f32 = keep.tile([P, P], F32)
+        make_identity(nc, ident_f32[:])
+        ident_bf16 = keep.tile([P, P], BF16)
+        make_identity(nc, ident_bf16[:])
+        b1_rows = keep.tile([P, P], BF16)
+        nc.vector.memset(b1_rows[:], 0.0)
+
+        raw = {}
+
+        def load_block(b):
+            if b < F_BLOCKS:
+                rows = raw_pool.tile([P, D_PASSES, PACK, K_PASS], BF16, name="raw")
+                for c in range(D_PASSES):
+                    nc.sync.dma_start(
+                        out=rows[:, c],
+                        in_=W1[
+                            c * K_PASS : (c + 1) * K_PASS, b * K_PASS : (b + 1) * K_PASS
+                        ].rearrange("(p j) x -> p j x", j=PACK),
+                    )
+            else:
+                g = b - F_BLOCKS
+                rows = raw_pool.tile([P, PACK, D], BF16, name="raw")
+                nc.sync.dma_start(
+                    out=rows[:],
+                    in_=W2[g * K_PASS : (g + 1) * K_PASS, :].rearrange("(j p) x -> p j x", p=P),
+                )
+            raw[b] = rows
+
+        load_block(0)
+        h_sb = keep.tile([P, TOK_TILES, D], BF16)
+        nc.sync.dma_start(out=h_sb[:], in_=h_rows.rearrange("(m p) d -> p m d", p=P))
+        nc.sync.dma_start(out=b1_rows[0 : F // P, :], in_=b1.rearrange("(i p) -> i p", p=P))
+        for b in range(1, AHEAD):
+            load_block(b)
+        b2_all = keep.tile([P, D], BF16)
+        nc.sync.dma_start(out=b2_all[:], in_=b2.partition_broadcast(P))
+        g2_all = keep.tile([P, D], BF16)
+        nc.sync.dma_start(out=g2_all[:], in_=g2.partition_broadcast(P))
+        beta2_all = keep.tile([P, D], BF16)
+        nc.sync.dma_start(out=beta2_all[:], in_=beta2.partition_broadcast(P))
+
+        def quantise_piece(engine_copy, rows):
+            grouped = grouped_pool.tile([P, K_PASS, PACK], BF16, name="grouped", align_bytes=64)
+            regroup(engine_copy, grouped[:], rows)
+            codes = codes_pool.tile([P, K_PASS], U32, name="codes", align_bytes=64)
+            scales = codes_pool.tile([P, K_PASS], U8, name="scales", align_bytes=64)
+            nc.vector.quantize_mx(
+                out=codes[:].bitcast(FP8X4),
+                scales=scales[:],
+                in_=grouped[:].rearrange("p w j -> p (w j)"),
+            )
+            return codes, scales
+
+        h_grouped = keep.tile([P, D_PASSES, TOK * PACK], BF16, align_bytes=64)
+        h_codes = keep.tile([P, D_PASSES, TOK], U32, align_bytes=64)
+        h_scales = keep.tile([P, D_PASSES, TOK], U8, align_bytes=64)
+        words_per_pass = K_PASS // 2
+        for c in range(D_PASSES):
+            for pair in range(TOK_TILES // 2):
+                xt = psum.tile([P, 2, 2, P], F32, name="xt", tag="bank")
+                for mm in range(2):
+                    h_words = h_sb[:, 2 * pair + mm, :].bitcast(F32)
+                    for u in range(2):
+                        nc.tensor.transpose(
+                            xt[:, mm, u, :],
+                            h_words[:, c * words_per_pass + u : (c + 1) * words_per_pass : 2],
+                            ident_f32[:],
+                        )
+                dst = (
+                    h_grouped[:, c, pair * 2 * P * PACK : (pair + 1) * 2 * P * PACK]
+                    .bitcast(F32)
+                    .rearrange("p (m k u) -> p m k u", m=2, u=2)
+                )
+                src = xt[:].rearrange("p m u k -> p m k u")
+                if pair == 0:
+                    nc.vector.tensor_copy(out=dst, in_=src)
+                else:
+                    nc.scalar.copy(out=dst, in_=src)
+        for c in range(D_PASSES):
+            nc.vector.quantize_mx(
+                out=h_codes[:, c, :].bitcast(FP8X4),
+                scales=h_scales[:, c, :],
+                in_=h_grouped[:, c, :],
+            )
+
+        b1_t = psum.tile([P, P], BF16, name="b1_t", tag="bank")
+        nc.tensor.transpose(b1_t[:], b1_rows[:], ident_bf16[:])
+        b1_cols = keep.tile([P, F // P], F32)
+        nc.vector.tensor_copy(out=b1_cols[:], in_=b1_t[:, 0 : F // P])
+
+        hid_codes = keep.tile([P, F_BLOCKS, TOK], U32, align_bytes=64)
+        hid_scales = keep.tile([P, F_BLOCKS, TOK], U8, align_bytes=64)
+        hb = keep.tile([P, TOK_TILES, D], F32)
+        for g in range(F_BLOCKS):
+            load_block(g + AHEAD)
+            w1_q = [
+                quantise_piece(nc.vector.tensor_copy, raw[g][:, 0]),
+                quantise_piece(nc.scalar.copy, raw[g][:, 1]),
+            ]
+            hid_bf = hid_pool.tile([P, PACK, TOK], BF16, name="hid_bf")
+            for j in range(PACK):
+                cols = slice(j * P, (j + 1) * P)
+                acc = psum.tile([P, TOK], F32, name="acc", tag="bank")
+                for c in range(D_PASSES):
+                    codes, scales = w1_q[c]
+                    nc.tensor.matmul_mx(
+                        out=acc[:],
+                        lhsT=codes[:, cols].bitcast(FP8X4),
+                        lhsT_scale=scales[:, cols],
+                        rhs=h_codes[:, c, :].bitcast(FP8X4),
+                        rhs_scale=h_scales[:, c, :],
+                        start=(c == 0),
+                        stop=(c == D_PASSES - 1),
+                    )
+                i = g * PACK + j
+                nc.scalar.activation(
+                    out=hid_bf[:, j, :], in_=acc[:], func=ACT.Relu,
+                    bias=b1_cols[:, i : i + 1], scale=1.0,
+                )
+            hid_grouped = grouped_pool.tile([P, TOK, PACK], BF16, name="grouped", align_bytes=64)
+            regroup(nc.vector.tensor_copy, hid_grouped[:], hid_bf[:])
+            nc.vector.quantize_mx(
+                out=hid_codes[:, g, :].bitcast(FP8X4),
+                scales=hid_scales[:, g, :],
+                in_=hid_grouped[:].rearrange("p w j -> p (w j)"),
+            )
+            if g % 2 == 1:
+                m = g // 2
+                nc.vector.tensor_tensor(
+                    out=hb[:, m, :], in0=h_sb[:, m, :], in1=b2_all[:], op=ALU.add
+                )
+
+        out_acc = {}
+        for m in range(TOK_TILES):
+            for n in range(D_HALVES):
+                out_acc[(m, n)] = psum.tile([P, N_TILE], F32, name="out_acc", tag="bank")
+        for g in range(F_BLOCKS):
+            if g + AHEAD < F_BLOCKS:
+                load_block(F_BLOCKS + g + AHEAD)
+            for n in range(D_HALVES):
+                engine_copy = nc.vector.tensor_copy if n == 0 else nc.scalar.copy
+                codes, scales = quantise_piece(
+                    engine_copy, raw[F_BLOCKS + g][:, :, n * N_TILE : (n + 1) * N_TILE]
+                )
+                for m in range(TOK_TILES):
+                    toks = slice(m * P, (m + 1) * P)
+                    nc.tensor.matmul_mx(
+                        out=out_acc[(m, n)][:],
+                        lhsT=hid_codes[:, g, toks].bitcast(FP8X4),
+                        lhsT_scale=hid_scales[:, g, toks],
+                        rhs=codes[:].bitcast(FP8X4),
+                        rhs_scale=scales[:],
+                        start=(g == 0),
+                        stop=(g == F_BLOCKS - 1),
+                    )
+
+        for m in range(TOK_TILES):
+            r = norm_pool.tile([P, D], F32, name="r")
+            r_sum = norm_pool.tile([P, D_HALVES], F32, name="r_sum")
+            for n in range(D_HALVES):
+                half = slice(n * N_TILE, (n + 1) * N_TILE)
+                nc.vector.scalar_tensor_tensor(
+                    out=r[:, half], in0=out_acc[(m, n)][:], scalar=1.0, in1=hb[:, m, half],
+                    op0=ALU.mult, op1=ALU.add, accum_out=r_sum[:, n : n + 1],
+                )
+            neg_mean = norm_pool.tile([P, 1], F32, name="neg_mean")
+            nc.vector.tensor_scalar(
+                out=neg_mean[:], in0=r_sum[:, 0:1], scalar1=r_sum[:, 1:2], scalar2=-1.0 / D,
+                op0=ALU.add, op1=ALU.mult,
+            )
+            squares = norm_pool.tile([P, D], BF16, name="squares", bufs=2)
+            sq_sum = norm_pool.tile([P, 1], F32, name="sq_sum")
+            nc.scalar.activation(
+                out=squares[:], in_=r[:], func=ACT.Square, bias=neg_mean[:], scale=1.0,
+                accum_out=sq_sum[:],
+            )
+            std = norm_pool.tile([P, 1], F32, name="std")
+            nc.scalar.activation(
+                out=std[:], in_=sq_sum[:], func=ACT.Sqrt, bias=eps_col[:], scale=1.0 / D
+            )
+            rstd = norm_pool.tile([P, 1], F32, name="rstd")
+            nc.vector.reciprocal(out=rstd[:], in_=std[:])
+            y = norm_pool.tile([P, D], F32, name="y")
+            nc.vector.scalar_tensor_tensor(
+                out=y[:], in0=r[:], scalar=neg_mean[:], in1=g2_all[:], op0=ALU.add, op1=ALU.mult
+            )
+            nc.vector.scalar_tensor_tensor(
+                out=y[:], in0=y[:], scalar=rstd[:], in1=beta2_all[:], op0=ALU.mult, op1=ALU.add
+            )
+            nc.sync.dma_start(out=out_rows[m * P : (m + 1) * P, :], in_=y[:])

@@ -23,6 +23,7 @@ TOK_TILES = TOK // P
 D_PASSES = D // K_PASS
 F_BLOCKS = F // K_PASS
 D_HALVES = D // N_TILE
+W_BLOCKS = 2 * F_BLOCKS
 AHEAD = 8
 
 FLOPS = 2 * TOK * D * F * 2
@@ -43,11 +44,12 @@ def tile_ffnn_encoder_pc_kernel(tc, h_attn, W1, b1, W2, b2, g2, beta2, out):
     with ExitStack() as ctx:
         keep = ctx.enter_context(tc.tile_pool(name="keep", bufs=1))
         raw_pool = ctx.enter_context(tc.tile_pool(name="raw", bufs=AHEAD + 1))
-        grouped_pool = ctx.enter_context(tc.tile_pool(name="grouped", bufs=4))
+        grouped_pool = ctx.enter_context(tc.tile_pool(name="grouped", bufs=6))
         codes_pool = ctx.enter_context(tc.tile_pool(name="codes", bufs=6))
         hid_pool = ctx.enter_context(tc.tile_pool(name="hid", bufs=3))
         norm_pool = ctx.enter_context(tc.tile_pool(name="norm", bufs=4))
         psum = ctx.enter_context(tc.psum_pool(name="psum", bufs=8))
+        ctx.enter_context(tc.manual_schedule())
 
         eps_col = keep.tile([P, 1], F32)
         nc.vector.memset(eps_col[:], EPS)
@@ -72,6 +74,7 @@ def tile_ffnn_encoder_pc_kernel(tc, h_attn, W1, b1, W2, b2, g2, beta2, out):
                             c * K_PASS : (c + 1) * K_PASS, b * K_PASS : (b + 1) * K_PASS
                         ].rearrange("(p j) x -> p j x", j=PACK),
                     )
+                raw[b] = [rows[:, c] for c in range(D_PASSES)]
             else:
                 g = b - F_BLOCKS
                 rows = raw_pool.tile([P, PACK, D], BF16, name="raw")
@@ -79,85 +82,63 @@ def tile_ffnn_encoder_pc_kernel(tc, h_attn, W1, b1, W2, b2, g2, beta2, out):
                     out=rows[:],
                     in_=W2[g * K_PASS : (g + 1) * K_PASS, :].rearrange("(j p) x -> p j x", p=P),
                 )
-            raw[b] = rows
+                raw[b] = [rows[:, :, n * N_TILE : (n + 1) * N_TILE] for n in range(D_HALVES)]
 
         load_block(0)
         h_sb = keep.tile([P, TOK_TILES, D], BF16)
-        nc.sync.dma_start(out=h_sb[:], in_=h_rows.rearrange("(m p) d -> p m d", p=P))
+        h_view = h_rows.rearrange("(m p) d -> p m d", p=P)
+        for pair in range(TOK_TILES // 2):
+            nc.sync.dma_start(
+                out=h_sb[:, 2 * pair : 2 * pair + 2, :], in_=h_view[:, 2 * pair : 2 * pair + 2, :]
+            )
         nc.sync.dma_start(out=b1_rows[0 : F // P, :], in_=b1.rearrange("(i p) -> i p", p=P))
-        for b in range(1, AHEAD):
-            load_block(b)
+        load_block(1)
         b2_all = keep.tile([P, D], BF16)
         nc.sync.dma_start(out=b2_all[:], in_=b2.partition_broadcast(P))
+        for b in range(2, AHEAD):
+            load_block(b)
         g2_all = keep.tile([P, D], BF16)
         nc.sync.dma_start(out=g2_all[:], in_=g2.partition_broadcast(P))
         beta2_all = keep.tile([P, D], BF16)
         nc.sync.dma_start(out=beta2_all[:], in_=beta2.partition_broadcast(P))
 
-        def quantise_piece(engine_copy, rows):
-            grouped = grouped_pool.tile([P, K_PASS, PACK], BF16, name="grouped", align_bytes=64)
-            regroup(engine_copy, grouped[:], rows)
+        grouped = {}
+        packed = {}
+
+        def regroup_piece(b, piece, engine_copy):
+            tile_ = grouped_pool.tile([P, K_PASS, PACK], BF16, name="grouped", align_bytes=64)
+            regroup(engine_copy, tile_[:], raw[b][piece])
+            grouped[(b, piece)] = tile_
+
+        def quantise_piece(b, piece):
             codes = codes_pool.tile([P, K_PASS], U32, name="codes", align_bytes=64)
             scales = codes_pool.tile([P, K_PASS], U8, name="scales", align_bytes=64)
             nc.vector.quantize_mx(
                 out=codes[:].bitcast(FP8X4),
                 scales=scales[:],
-                in_=grouped[:].rearrange("p w j -> p (w j)"),
+                in_=grouped[(b, piece)][:].rearrange("p w j -> p (w j)"),
             )
-            return codes, scales
+            packed[(b, piece)] = (codes, scales)
 
         h_grouped = keep.tile([P, D_PASSES, TOK * PACK], BF16, align_bytes=64)
         h_codes = keep.tile([P, D_PASSES, TOK], U32, align_bytes=64)
         h_scales = keep.tile([P, D_PASSES, TOK], U8, align_bytes=64)
-        words_per_pass = K_PASS // 2
-        for c in range(D_PASSES):
-            for pair in range(TOK_TILES // 2):
-                xt = psum.tile([P, 2, 2, P], F32, name="xt", tag="bank")
-                for mm in range(2):
-                    h_words = h_sb[:, 2 * pair + mm, :].bitcast(F32)
-                    for u in range(2):
-                        nc.tensor.transpose(
-                            xt[:, mm, u, :],
-                            h_words[:, c * words_per_pass + u : (c + 1) * words_per_pass : 2],
-                            ident_f32[:],
-                        )
-                dst = (
-                    h_grouped[:, c, pair * 2 * P * PACK : (pair + 1) * 2 * P * PACK]
-                    .bitcast(F32)
-                    .rearrange("p (m k u) -> p m k u", m=2, u=2)
-                )
-                src = xt[:].rearrange("p m u k -> p m k u")
-                if pair == 0:
-                    nc.vector.tensor_copy(out=dst, in_=src)
-                else:
-                    nc.scalar.copy(out=dst, in_=src)
-        for c in range(D_PASSES):
-            nc.vector.quantize_mx(
-                out=h_codes[:, c, :].bitcast(FP8X4),
-                scales=h_scales[:, c, :],
-                in_=h_grouped[:, c, :],
-            )
-
-        b1_t = psum.tile([P, P], BF16, name="b1_t", tag="bank")
-        nc.tensor.transpose(b1_t[:], b1_rows[:], ident_bf16[:])
         b1_cols = keep.tile([P, F // P], F32)
-        nc.vector.tensor_copy(out=b1_cols[:], in_=b1_t[:, 0 : F // P])
-
         hid_codes = keep.tile([P, F_BLOCKS, TOK], U32, align_bytes=64)
         hid_scales = keep.tile([P, F_BLOCKS, TOK], U8, align_bytes=64)
         hb = keep.tile([P, TOK_TILES, D], F32)
-        for g in range(F_BLOCKS):
-            load_block(g + AHEAD)
-            w1_q = [
-                quantise_piece(nc.vector.tensor_copy, raw[g][:, 0]),
-                quantise_piece(nc.scalar.copy, raw[g][:, 1]),
-            ]
-            hid_bf = hid_pool.tile([P, PACK, TOK], BF16, name="hid_bf")
+        hid_acc = {}
+        hid_bf = {}
+        hid_grouped = {}
+        out_acc = {}
+
+        def first_matmul(g):
+            hid_acc[g] = []
             for j in range(PACK):
                 cols = slice(j * P, (j + 1) * P)
                 acc = psum.tile([P, TOK], F32, name="acc", tag="bank")
                 for c in range(D_PASSES):
-                    codes, scales = w1_q[c]
+                    codes, scales = packed[(g, c)]
                     nc.tensor.matmul_mx(
                         out=acc[:],
                         lhsT=codes[:, cols].bitcast(FP8X4),
@@ -167,79 +148,156 @@ def tile_ffnn_encoder_pc_kernel(tc, h_attn, W1, b1, W2, b2, g2, beta2, out):
                         start=(c == 0),
                         stop=(c == D_PASSES - 1),
                     )
+                hid_acc[g].append(acc)
+
+        def relu_block(g):
+            hid_bf[g] = hid_pool.tile([P, PACK, TOK], BF16, name="hid_bf")
+            for j in range(PACK):
                 i = g * PACK + j
                 nc.scalar.activation(
-                    out=hid_bf[:, j, :], in_=acc[:], func=ACT.Relu,
+                    out=hid_bf[g][:, j, :], in_=hid_acc[g][j][:], func=ACT.Relu,
                     bias=b1_cols[:, i : i + 1], scale=1.0,
                 )
-            hid_grouped = grouped_pool.tile([P, TOK, PACK], BF16, name="grouped", align_bytes=64)
-            regroup(nc.vector.tensor_copy, hid_grouped[:], hid_bf[:])
+
+        def regroup_hid(g):
+            hid_grouped[g] = grouped_pool.tile(
+                [P, TOK, PACK], BF16, name="grouped", align_bytes=64
+            )
+            regroup(nc.vector.tensor_copy, hid_grouped[g][:], hid_bf[g][:])
+
+        def quantise_hid(g):
             nc.vector.quantize_mx(
                 out=hid_codes[:, g, :].bitcast(FP8X4),
                 scales=hid_scales[:, g, :],
-                in_=hid_grouped[:].rearrange("p w j -> p (w j)"),
+                in_=hid_grouped[g][:].rearrange("p w j -> p (w j)"),
             )
-            if g % 2 == 1:
-                m = g // 2
-                nc.vector.tensor_tensor(
-                    out=hb[:, m, :], in0=h_sb[:, m, :], in1=b2_all[:], op=ALU.add
+
+        def second_matmul(g, n):
+            codes, scales = packed[(F_BLOCKS + g, n)]
+            for m in range(TOK_TILES):
+                if g == 0:
+                    out_acc[(m, n)] = psum.tile([P, N_TILE], F32, name="out_acc", tag="bank")
+                toks = slice(m * P, (m + 1) * P)
+                nc.tensor.matmul_mx(
+                    out=out_acc[(m, n)][:],
+                    lhsT=hid_codes[:, g, toks].bitcast(FP8X4),
+                    lhsT_scale=hid_scales[:, g, toks],
+                    rhs=codes[:].bitcast(FP8X4),
+                    rhs_scale=scales[:],
+                    start=(g == 0),
+                    stop=(g == F_BLOCKS - 1),
                 )
 
-        out_acc = {}
-        for m in range(TOK_TILES):
-            for n in range(D_HALVES):
-                out_acc[(m, n)] = psum.tile([P, N_TILE], F32, name="out_acc", tag="bank")
-        for g in range(F_BLOCKS):
-            if g + AHEAD < F_BLOCKS:
-                load_block(F_BLOCKS + g + AHEAD)
-            for n in range(D_HALVES):
-                engine_copy = nc.vector.tensor_copy if n == 0 else nc.scalar.copy
-                codes, scales = quantise_piece(
-                    engine_copy, raw[F_BLOCKS + g][:, :, n * N_TILE : (n + 1) * N_TILE]
-                )
-                for m in range(TOK_TILES):
-                    toks = slice(m * P, (m + 1) * P)
-                    nc.tensor.matmul_mx(
-                        out=out_acc[(m, n)][:],
-                        lhsT=hid_codes[:, g, toks].bitcast(FP8X4),
-                        lhsT_scale=hid_scales[:, g, toks],
-                        rhs=codes[:].bitcast(FP8X4),
-                        rhs_scale=scales[:],
-                        start=(g == 0),
-                        stop=(g == F_BLOCKS - 1),
+        def prepare_h():
+            words_per_pass = K_PASS // 2
+            for pair in range(TOK_TILES // 2):
+                for c in range(D_PASSES):
+                    xt = psum.tile([P, 2, 2, P], F32, name="xt", tag="bank")
+                    for mm in range(2):
+                        h_words = h_sb[:, 2 * pair + mm, :].bitcast(F32)
+                        for u in range(2):
+                            nc.tensor.transpose(
+                                xt[:, mm, u, :],
+                                h_words[:, c * words_per_pass + u : (c + 1) * words_per_pass : 2],
+                                ident_f32[:],
+                            )
+                    dst = (
+                        h_grouped[:, c, pair * 2 * P * PACK : (pair + 1) * 2 * P * PACK]
+                        .bitcast(F32)
+                        .rearrange("p (m k u) -> p m k u", m=2, u=2)
                     )
+                    src = xt[:].rearrange("p m u k -> p m k u")
+                    if c == 0:
+                        nc.vector.tensor_copy(out=dst, in_=src)
+                    else:
+                        nc.scalar.copy(out=dst, in_=src)
+            b1_t = psum.tile([P, P], BF16, name="b1_t", tag="bank")
+            nc.tensor.transpose(b1_t[:], b1_rows[:], ident_bf16[:])
+            nc.vector.tensor_copy(out=b1_cols[:], in_=b1_t[:, 0 : F // P])
+            for c in range(D_PASSES):
+                nc.vector.quantize_mx(
+                    out=h_codes[:, c, :].bitcast(FP8X4),
+                    scales=h_scales[:, c, :],
+                    in_=h_grouped[:, c, :],
+                )
 
-        for m in range(TOK_TILES):
-            r = norm_pool.tile([P, D], F32, name="r")
+        for s in range(W_BLOCKS + 1):
+            if s + AHEAD < W_BLOCKS:
+                load_block(s + AHEAD)
+            if s < W_BLOCKS:
+                regroup_piece(s, 0, nc.vector.tensor_copy)
+                regroup_piece(s, 1, nc.scalar.copy)
+            if 0 <= s - 3 < F_BLOCKS:
+                regroup_hid(s - 3)
+            if s >= 1:
+                quantise_piece(s - 1, 1)
+            if s < W_BLOCKS:
+                quantise_piece(s, 0)
+            if s == 0:
+                prepare_h()
+            if 0 <= s - 2 < F_BLOCKS:
+                relu_block(s - 2)
+            if 0 <= s - 1 < F_BLOCKS:
+                first_matmul(s - 1)
+            if s - 1 >= F_BLOCKS:
+                second_matmul(s - 1 - F_BLOCKS, 1)
+            if F_BLOCKS <= s < W_BLOCKS:
+                second_matmul(s - F_BLOCKS, 0)
+            if 0 <= s - 3 < F_BLOCKS:
+                quantise_hid(s - 3)
+                m, n = divmod(s - 3, D_HALVES)
+                half = slice(n * N_TILE, (n + 1) * N_TILE)
+                nc.vector.tensor_tensor(
+                    out=hb[:, m, half], in0=h_sb[:, m, half], in1=b2_all[:, half], op=ALU.add
+                )
+
+        r = {}
+        neg_mean = {}
+        rstd = {}
+        y = {}
+
+        def residual(m):
+            r[m] = norm_pool.tile([P, D], F32, name="r")
             r_sum = norm_pool.tile([P, D_HALVES], F32, name="r_sum")
             for n in range(D_HALVES):
                 half = slice(n * N_TILE, (n + 1) * N_TILE)
                 nc.vector.scalar_tensor_tensor(
-                    out=r[:, half], in0=out_acc[(m, n)][:], scalar=1.0, in1=hb[:, m, half],
+                    out=r[m][:, half], in0=out_acc[(m, n)][:], scalar=1.0, in1=hb[:, m, half],
                     op0=ALU.mult, op1=ALU.add, accum_out=r_sum[:, n : n + 1],
                 )
-            neg_mean = norm_pool.tile([P, 1], F32, name="neg_mean")
+            neg_mean[m] = norm_pool.tile([P, 1], F32, name="neg_mean")
             nc.vector.tensor_scalar(
-                out=neg_mean[:], in0=r_sum[:, 0:1], scalar1=r_sum[:, 1:2], scalar2=-1.0 / D,
+                out=neg_mean[m][:], in0=r_sum[:, 0:1], scalar1=r_sum[:, 1:2], scalar2=-1.0 / D,
                 op0=ALU.add, op1=ALU.mult,
             )
             squares = norm_pool.tile([P, D], BF16, name="squares", bufs=2)
             sq_sum = norm_pool.tile([P, 1], F32, name="sq_sum")
             nc.scalar.activation(
-                out=squares[:], in_=r[:], func=ACT.Square, bias=neg_mean[:], scale=1.0,
+                out=squares[:], in_=r[m][:], func=ACT.Square, bias=neg_mean[m][:], scale=1.0,
                 accum_out=sq_sum[:],
             )
             std = norm_pool.tile([P, 1], F32, name="std")
             nc.scalar.activation(
                 out=std[:], in_=sq_sum[:], func=ACT.Sqrt, bias=eps_col[:], scale=1.0 / D
             )
-            rstd = norm_pool.tile([P, 1], F32, name="rstd")
-            nc.vector.reciprocal(out=rstd[:], in_=std[:])
-            y = norm_pool.tile([P, D], F32, name="y")
+            return std
+
+        def normalise(m, std):
+            y[m] = norm_pool.tile([P, D], F32, name="y")
             nc.vector.scalar_tensor_tensor(
-                out=y[:], in0=r[:], scalar=neg_mean[:], in1=g2_all[:], op0=ALU.add, op1=ALU.mult
+                out=y[m][:], in0=r[m][:], scalar=neg_mean[m][:], in1=g2_all[:],
+                op0=ALU.add, op1=ALU.mult,
             )
+            rstd[m] = norm_pool.tile([P, 1], F32, name="rstd")
+            nc.vector.reciprocal(out=rstd[m][:], in_=std[:])
             nc.vector.scalar_tensor_tensor(
-                out=y[:], in0=y[:], scalar=rstd[:], in1=beta2_all[:], op0=ALU.mult, op1=ALU.add
+                out=y[m][:], in0=y[m][:], scalar=rstd[m][:], in1=beta2_all[:],
+                op0=ALU.mult, op1=ALU.add,
             )
-            nc.sync.dma_start(out=out_rows[m * P : (m + 1) * P, :], in_=y[:])
+            nc.sync.dma_start(out=out_rows[m * P : (m + 1) * P, :], in_=y[m][:])
+
+        stds = {0: residual(0)}
+        for m in range(TOK_TILES):
+            if m + 1 < TOK_TILES:
+                stds[m + 1] = residual(m + 1)
+            normalise(m, stds[m])

@@ -25,6 +25,7 @@ F_BLOCKS = F // K_PASS
 D_HALVES = D // N_TILE
 W_BLOCKS = 2 * F_BLOCKS
 AHEAD = 8
+VECTOR_EXTRA_COLS = 64
 
 FLOPS = 2 * TOK * D * F * 2
 
@@ -61,6 +62,10 @@ def tile_ffnn_encoder_pc_kernel(tc, h_attn, W1, b1, W2, b2, g2, beta2, out):
         make_identity(nc, ident_bf16[:])
         b1_rows = keep.tile([P, P], BF16)
         nc.vector.memset(b1_rows[:], 0.0)
+        ones_bf16 = keep.tile([P, P], BF16)
+        nc.vector.memset(ones_bf16[:], 1.0)
+        b2_rows = keep.tile([P, D], BF16)
+        nc.vector.memset(b2_rows[:], 0.0)
 
         raw = {}
 
@@ -92,11 +97,9 @@ def tile_ffnn_encoder_pc_kernel(tc, h_attn, W1, b1, W2, b2, g2, beta2, out):
                 out=h_sb[:, 2 * pair : 2 * pair + 2, :], in_=h_view[:, 2 * pair : 2 * pair + 2, :]
             )
         nc.sync.dma_start(out=b1_rows[0 : F // P, :], in_=b1.rearrange("(i p) -> i p", p=P))
-        load_block(1)
-        b2_all = keep.tile([P, D], BF16)
-        nc.sync.dma_start(out=b2_all[:], in_=b2.partition_broadcast(P))
-        for b in range(2, AHEAD):
+        for b in range(1, AHEAD):
             load_block(b)
+        nc.sync.dma_start(out=b2_rows[0:1, :], in_=b2.rearrange("(o d) -> o d", o=1))
         g2_all = keep.tile([P, D], BF16)
         nc.sync.dma_start(out=g2_all[:], in_=g2.partition_broadcast(P))
         beta2_all = keep.tile([P, D], BF16)
@@ -105,10 +108,18 @@ def tile_ffnn_encoder_pc_kernel(tc, h_attn, W1, b1, W2, b2, g2, beta2, out):
         grouped = {}
         packed = {}
 
-        def regroup_piece(b, piece, engine_copy):
-            tile_ = grouped_pool.tile([P, K_PASS, PACK], BF16, name="grouped", align_bytes=64)
-            regroup(engine_copy, tile_[:], raw[b][piece])
-            grouped[(b, piece)] = tile_
+        def regroup_block(b):
+            for piece in range(2):
+                grouped[(b, piece)] = grouped_pool.tile(
+                    [P, K_PASS, PACK], BF16, name="grouped", align_bytes=64
+                )
+            split = VECTOR_EXTRA_COLS if b < F_BLOCKS else 0
+            regroup(nc.vector.tensor_copy, grouped[(b, 0)][:], raw[b][0])
+            if split > 0:
+                regroup(
+                    nc.vector.tensor_copy, grouped[(b, 1)][:, :split, :], raw[b][1][:, :, :split]
+                )
+            regroup(nc.scalar.copy, grouped[(b, 1)][:, split:, :], raw[b][1][:, :, split:])
 
         def quantise_piece(b, piece):
             codes = codes_pool.tile([P, K_PASS], U32, name="codes", align_bytes=64)
@@ -126,7 +137,6 @@ def tile_ffnn_encoder_pc_kernel(tc, h_attn, W1, b1, W2, b2, g2, beta2, out):
         b1_cols = keep.tile([P, F // P], F32)
         hid_codes = keep.tile([P, F_BLOCKS, TOK], U32, align_bytes=64)
         hid_scales = keep.tile([P, F_BLOCKS, TOK], U8, align_bytes=64)
-        hb = keep.tile([P, TOK_TILES, D], F32)
         hid_acc = {}
         hid_bf = {}
         hid_grouped = {}
@@ -221,18 +231,15 @@ def tile_ffnn_encoder_pc_kernel(tc, h_attn, W1, b1, W2, b2, g2, beta2, out):
                     in_=h_grouped[:, c, :],
                 )
 
-        for s in range(W_BLOCKS + 1):
+        for s in range(W_BLOCKS):
             if s + AHEAD < W_BLOCKS:
                 load_block(s + AHEAD)
-            if s < W_BLOCKS:
-                regroup_piece(s, 0, nc.vector.tensor_copy)
-                regroup_piece(s, 1, nc.scalar.copy)
-            if 0 <= s - 3 < F_BLOCKS:
-                regroup_hid(s - 3)
+            regroup_block(s)
             if s >= 1:
                 quantise_piece(s - 1, 1)
-            if s < W_BLOCKS:
-                quantise_piece(s, 0)
+            if 0 <= s - 3 < F_BLOCKS:
+                regroup_hid(s - 3)
+            quantise_piece(s, 0)
             if s == 0:
                 prepare_h()
             if 0 <= s - 2 < F_BLOCKS:
@@ -241,34 +248,46 @@ def tile_ffnn_encoder_pc_kernel(tc, h_attn, W1, b1, W2, b2, g2, beta2, out):
                 first_matmul(s - 1)
             if s - 1 >= F_BLOCKS:
                 second_matmul(s - 1 - F_BLOCKS, 1)
-            if F_BLOCKS <= s < W_BLOCKS:
+            if s >= F_BLOCKS:
                 second_matmul(s - F_BLOCKS, 0)
             if 0 <= s - 3 < F_BLOCKS:
                 quantise_hid(s - 3)
-                m, n = divmod(s - 3, D_HALVES)
-                half = slice(n * N_TILE, (n + 1) * N_TILE)
-                nc.vector.tensor_tensor(
-                    out=hb[:, m, half], in0=h_sb[:, m, half], in1=b2_all[:, half], op=ALU.add
-                )
 
         r = {}
+        r_sum = {}
         neg_mean = {}
-        rstd = {}
-        y = {}
-
-        def residual(m):
+        std = {}
+        for m in range(TOK_TILES):
             r[m] = norm_pool.tile([P, D], F32, name="r")
-            r_sum = norm_pool.tile([P, D_HALVES], F32, name="r_sum")
-            for n in range(D_HALVES):
-                half = slice(n * N_TILE, (n + 1) * N_TILE)
-                nc.vector.scalar_tensor_tensor(
-                    out=r[m][:, half], in0=out_acc[(m, n)][:], scalar=1.0, in1=hb[:, m, half],
-                    op0=ALU.mult, op1=ALU.add, accum_out=r_sum[:, n : n + 1],
-                )
+            r_sum[m] = norm_pool.tile([P, D_HALVES], F32, name="r_sum")
+
+        hb = {}
+
+        def empty_bank(m, n):
+            half = slice(n * N_TILE, (n + 1) * N_TILE)
+            nc.scalar.copy(out=r[m][:, half], in_=out_acc[(m, n)][:])
+            hb[(m, n)] = psum.tile([P, N_TILE], F32, name="hb", tag="bank")
+            nc.tensor.matmul(
+                out=hb[(m, n)][:], lhsT=ident_bf16[:], rhs=h_sb[:, m, half],
+                start=True, stop=False,
+            )
+            nc.tensor.matmul(
+                out=hb[(m, n)][:], lhsT=ones_bf16[:], rhs=b2_rows[:, half],
+                start=False, stop=True,
+            )
+
+        def add_residual(m, n):
+            half = slice(n * N_TILE, (n + 1) * N_TILE)
+            nc.vector.scalar_tensor_tensor(
+                out=r[m][:, half], in0=hb[(m, n)][:], scalar=1.0, in1=r[m][:, half],
+                op0=ALU.mult, op1=ALU.add, accum_out=r_sum[m][:, n : n + 1],
+            )
+
+        def statistics(m):
             neg_mean[m] = norm_pool.tile([P, 1], F32, name="neg_mean")
             nc.vector.tensor_scalar(
-                out=neg_mean[m][:], in0=r_sum[:, 0:1], scalar1=r_sum[:, 1:2], scalar2=-1.0 / D,
-                op0=ALU.add, op1=ALU.mult,
+                out=neg_mean[m][:], in0=r_sum[m][:, 0:1], scalar1=r_sum[m][:, 1:2],
+                scalar2=-1.0 / D, op0=ALU.add, op1=ALU.mult,
             )
             squares = norm_pool.tile([P, D], BF16, name="squares", bufs=2)
             sq_sum = norm_pool.tile([P, 1], F32, name="sq_sum")
@@ -276,28 +295,38 @@ def tile_ffnn_encoder_pc_kernel(tc, h_attn, W1, b1, W2, b2, g2, beta2, out):
                 out=squares[:], in_=r[m][:], func=ACT.Square, bias=neg_mean[m][:], scale=1.0,
                 accum_out=sq_sum[:],
             )
-            std = norm_pool.tile([P, 1], F32, name="std")
+            std[m] = norm_pool.tile([P, 1], F32, name="std")
             nc.scalar.activation(
-                out=std[:], in_=sq_sum[:], func=ACT.Sqrt, bias=eps_col[:], scale=1.0 / D
+                out=std[m][:], in_=sq_sum[:], func=ACT.Sqrt, bias=eps_col[:], scale=1.0 / D
             )
-            return std
 
-        def normalise(m, std):
-            y[m] = norm_pool.tile([P, D], F32, name="y")
+        def normalise(m):
+            y = norm_pool.tile([P, D], F32, name="y")
             nc.vector.scalar_tensor_tensor(
-                out=y[m][:], in0=r[m][:], scalar=neg_mean[m][:], in1=g2_all[:],
+                out=y[:], in0=r[m][:], scalar=neg_mean[m][:], in1=g2_all[:],
                 op0=ALU.add, op1=ALU.mult,
             )
-            rstd[m] = norm_pool.tile([P, 1], F32, name="rstd")
-            nc.vector.reciprocal(out=rstd[m][:], in_=std[:])
-            nc.vector.scalar_tensor_tensor(
-                out=y[m][:], in0=y[m][:], scalar=rstd[m][:], in1=beta2_all[:],
-                op0=ALU.mult, op1=ALU.add,
-            )
-            nc.sync.dma_start(out=out_rows[m * P : (m + 1) * P, :], in_=y[m][:])
+            rstd = norm_pool.tile([P, 1], F32, name="rstd")
+            nc.vector.reciprocal(out=rstd[:], in_=std[m][:])
+            for n in range(D_HALVES):
+                half = slice(n * N_TILE, (n + 1) * N_TILE)
+                nc.vector.scalar_tensor_tensor(
+                    out=y[:, half], in0=y[:, half], scalar=rstd[:], in1=beta2_all[:, half],
+                    op0=ALU.mult, op1=ALU.add,
+                )
+                nc.sync.dma_start(out=out_rows[m * P : (m + 1) * P, half], in_=y[:, half])
 
-        stds = {0: residual(0)}
+        quantise_piece(W_BLOCKS - 1, 1)
+        second_matmul(F_BLOCKS - 1, 1)
+        for n in range(D_HALVES):
+            for m in range(TOK_TILES):
+                empty_bank(m, n)
+        for m in range(TOK_TILES):
+            add_residual(m, 0)
+        add_residual(0, 1)
+        statistics(0)
         for m in range(TOK_TILES):
             if m + 1 < TOK_TILES:
-                stds[m + 1] = residual(m + 1)
-            normalise(m, stds[m])
+                add_residual(m + 1, 1)
+                statistics(m + 1)
+            normalise(m)

@@ -24,8 +24,8 @@ D_PASSES = D // K_PASS
 F_BLOCKS = F // K_PASS
 D_HALVES = D // N_TILE
 W_BLOCKS = 2 * F_BLOCKS
-AHEAD = 8
-VECTOR_EXTRA_COLS = 64
+AHEAD = 7
+VECTOR_EXTRA_COLS = 160
 
 FLOPS = 2 * TOK * D * F * 2
 
@@ -97,9 +97,9 @@ def tile_ffnn_encoder_pc_kernel(tc, h_attn, W1, b1, W2, b2, g2, beta2, out):
                 out=h_sb[:, 2 * pair : 2 * pair + 2, :], in_=h_view[:, 2 * pair : 2 * pair + 2, :]
             )
         nc.sync.dma_start(out=b1_rows[0 : F // P, :], in_=b1.rearrange("(i p) -> i p", p=P))
+        nc.sync.dma_start(out=b2_rows[0:1, :], in_=b2.rearrange("(o d) -> o d", o=1))
         for b in range(1, AHEAD):
             load_block(b)
-        nc.sync.dma_start(out=b2_rows[0:1, :], in_=b2.rearrange("(o d) -> o d", o=1))
         g2_all = keep.tile([P, D], BF16)
         nc.sync.dma_start(out=g2_all[:], in_=g2.partition_broadcast(P))
         beta2_all = keep.tile([P, D], BF16)
@@ -231,6 +231,25 @@ def tile_ffnn_encoder_pc_kernel(tc, h_attn, W1, b1, W2, b2, g2, beta2, out):
                     in_=h_grouped[:, c, :],
                 )
 
+        hb = keep.tile([P, TOK_TILES, D], F32)
+        hb_acc = {}
+
+        def residual_matmul(m, n):
+            half = slice(n * N_TILE, (n + 1) * N_TILE)
+            hb_acc[(m, n)] = psum.tile([P, N_TILE], F32, name="hb_acc", tag="bank")
+            nc.tensor.matmul(
+                out=hb_acc[(m, n)][:], lhsT=ident_bf16[:], rhs=h_sb[:, m, half],
+                start=True, stop=False,
+            )
+            nc.tensor.matmul(
+                out=hb_acc[(m, n)][:], lhsT=ones_bf16[:], rhs=b2_rows[:, half],
+                start=False, stop=True,
+            )
+
+        def residual_copy(m, n):
+            half = slice(n * N_TILE, (n + 1) * N_TILE)
+            nc.scalar.copy(out=hb[:, m, half], in_=hb_acc[(m, n)][:])
+
         for s in range(W_BLOCKS):
             if s + AHEAD < W_BLOCKS:
                 load_block(s + AHEAD)
@@ -244,6 +263,8 @@ def tile_ffnn_encoder_pc_kernel(tc, h_attn, W1, b1, W2, b2, g2, beta2, out):
                 prepare_h()
             if 0 <= s - 2 < F_BLOCKS:
                 relu_block(s - 2)
+            if 0 <= s - 1 < TOK_TILES * D_HALVES:
+                residual_copy(*divmod(s - 1, D_HALVES))
             if 0 <= s - 1 < F_BLOCKS:
                 first_matmul(s - 1)
             if s - 1 >= F_BLOCKS:
@@ -252,34 +273,24 @@ def tile_ffnn_encoder_pc_kernel(tc, h_attn, W1, b1, W2, b2, g2, beta2, out):
                 second_matmul(s - F_BLOCKS, 0)
             if 0 <= s - 3 < F_BLOCKS:
                 quantise_hid(s - 3)
+            if s < TOK_TILES * D_HALVES:
+                residual_matmul(*divmod(s, D_HALVES))
+
+        quantise_piece(W_BLOCKS - 1, 1)
+        second_matmul(F_BLOCKS - 1, 1)
 
         r = {}
         r_sum = {}
         neg_mean = {}
         std = {}
-        for m in range(TOK_TILES):
-            r[m] = norm_pool.tile([P, D], F32, name="r")
-            r_sum[m] = norm_pool.tile([P, D_HALVES], F32, name="r_sum")
-
-        hb = {}
-
-        def empty_bank(m, n):
-            half = slice(n * N_TILE, (n + 1) * N_TILE)
-            nc.scalar.copy(out=r[m][:, half], in_=out_acc[(m, n)][:])
-            hb[(m, n)] = psum.tile([P, N_TILE], F32, name="hb", tag="bank")
-            nc.tensor.matmul(
-                out=hb[(m, n)][:], lhsT=ident_bf16[:], rhs=h_sb[:, m, half],
-                start=True, stop=False,
-            )
-            nc.tensor.matmul(
-                out=hb[(m, n)][:], lhsT=ones_bf16[:], rhs=b2_rows[:, half],
-                start=False, stop=True,
-            )
 
         def add_residual(m, n):
+            if n == 0:
+                r[m] = norm_pool.tile([P, D], F32, name="r")
+                r_sum[m] = norm_pool.tile([P, D_HALVES], F32, name="r_sum")
             half = slice(n * N_TILE, (n + 1) * N_TILE)
             nc.vector.scalar_tensor_tensor(
-                out=r[m][:, half], in0=hb[(m, n)][:], scalar=1.0, in1=r[m][:, half],
+                out=r[m][:, half], in0=out_acc[(m, n)][:], scalar=1.0, in1=hb[:, m, half],
                 op0=ALU.mult, op1=ALU.add, accum_out=r_sum[m][:, n : n + 1],
             )
 
@@ -316,11 +327,6 @@ def tile_ffnn_encoder_pc_kernel(tc, h_attn, W1, b1, W2, b2, g2, beta2, out):
                 )
                 nc.sync.dma_start(out=out_rows[m * P : (m + 1) * P, half], in_=y[:, half])
 
-        quantise_piece(W_BLOCKS - 1, 1)
-        second_matmul(F_BLOCKS - 1, 1)
-        for n in range(D_HALVES):
-            for m in range(TOK_TILES):
-                empty_bank(m, n)
         for m in range(TOK_TILES):
             add_residual(m, 0)
         add_residual(0, 1)

@@ -32,8 +32,8 @@ FLOPS = 2 * TOK * D * F * 2
 
 def regroup(engine_copy, grouped, rows):
     engine_copy(
-        out=grouped.rearrange("p (c i) j -> p c j i", i=4),
-        in_=rows.rearrange("p j (c i) -> p c j i", i=4),
+        out=grouped.rearrange("p (c i) j -> p c j i", i=8),
+        in_=rows.rearrange("p j (c i) -> p c j i", i=8),
     )
 
 

@@ -66,6 +66,10 @@ def tile_ffnn_encoder_pc_kernel(tc, h_attn, W1, b1, W2, b2, g2, beta2, out):
         nc.vector.memset(ones_bf16[:], 1.0)
         b2_rows = keep.tile([P, D], BF16)
         nc.vector.memset(b2_rows[:], 0.0)
+        g2_rows = keep.tile([P, D], BF16)
+        nc.vector.memset(g2_rows[:], 0.0)
+        beta2_rows = keep.tile([P, D], BF16)
+        nc.vector.memset(beta2_rows[:], 0.0)
 
         raw = {}
 
@@ -100,6 +104,8 @@ def tile_ffnn_encoder_pc_kernel(tc, h_attn, W1, b1, W2, b2, g2, beta2, out):
         nc.sync.dma_start(out=b2_rows[0:1, :], in_=b2.rearrange("(o d) -> o d", o=1))
         for b in range(1, AHEAD):
             load_block(b)
+        nc.sync.dma_start(out=g2_rows[0:1, :], in_=g2.rearrange("(o d) -> o d", o=1))
+        nc.sync.dma_start(out=beta2_rows[0:1, :], in_=beta2.rearrange("(o d) -> o d", o=1))
         g2_all = keep.tile([P, D], BF16)
         nc.sync.dma_start(out=g2_all[:], in_=g2.partition_broadcast(P))
         beta2_all = keep.tile([P, D], BF16)
@@ -311,28 +317,73 @@ def tile_ffnn_encoder_pc_kernel(tc, h_attn, W1, b1, W2, b2, g2, beta2, out):
                 out=std[m][:], in_=sq_sum[:], func=ACT.Sqrt, bias=eps_col[:], scale=1.0 / D
             )
 
+        norm_rows = {}
+
+        def spread_row(name, rows):
+            norm_rows[name] = []
+            for n in range(D_HALVES):
+                bank = psum.tile([P, N_TILE], F32, name=name, tag="bank")
+                nc.tensor.matmul(
+                    out=bank[:], lhsT=ones_bf16[:], rhs=rows[:, n * N_TILE : (n + 1) * N_TILE],
+                    start=True, stop=True,
+                )
+                norm_rows[name].append(bank)
+
+        def store(queue, m, n, y):
+            half = slice(n * N_TILE, (n + 1) * N_TILE)
+            queue.dma_start(out=out_rows[m * P : (m + 1) * P, half], in_=y[:, half])
+
         def normalise(m):
             y = norm_pool.tile([P, D], F32, name="y")
-            nc.vector.scalar_tensor_tensor(
-                out=y[:], in0=r[m][:], scalar=neg_mean[m][:], in1=g2_all[:],
-                op0=ALU.add, op1=ALU.mult,
-            )
+            for n in range(D_HALVES):
+                half = slice(n * N_TILE, (n + 1) * N_TILE)
+                nc.vector.scalar_tensor_tensor(
+                    out=y[:, half], in0=r[m][:, half], scalar=neg_mean[m][:],
+                    in1=norm_rows["g2_psum"][n][:], op0=ALU.add, op1=ALU.mult,
+                )
             rstd = norm_pool.tile([P, 1], F32, name="rstd")
             nc.vector.reciprocal(out=rstd[:], in_=std[m][:])
             for n in range(D_HALVES):
                 half = slice(n * N_TILE, (n + 1) * N_TILE)
                 nc.vector.scalar_tensor_tensor(
-                    out=y[:, half], in0=y[:, half], scalar=rstd[:], in1=beta2_all[:, half],
-                    op0=ALU.mult, op1=ALU.add,
+                    out=y[:, half], in0=y[:, half], scalar=rstd[:],
+                    in1=norm_rows["beta2_psum"][n][:], op0=ALU.mult, op1=ALU.add,
                 )
-                nc.sync.dma_start(out=out_rows[m * P : (m + 1) * P, half], in_=y[:, half])
+                store(nc.sync, m, n, y)
+
+        def normalise_without_vector(m):
+            rstd = norm_pool.tile([P, 1], F32, name="rstd")
+            nc.vector.reciprocal(out=rstd[:], in_=std[m][:])
+            shift = norm_pool.tile([P, 1], F32, name="shift", bufs=1)
+            nc.vector.tensor_scalar(
+                out=shift[:], in0=neg_mean[m][:], scalar1=rstd[:], scalar2=None, op0=ALU.mult
+            )
+            z = norm_pool.tile([P, D], F32, name="y")
+            nc.scalar.activation(
+                out=z[:], in_=r[m][:], func=ACT.Identity, bias=shift[:], scale=rstd[:]
+            )
+            for n in range(D_HALVES):
+                half = slice(n * N_TILE, (n + 1) * N_TILE)
+                for op, rows in ((ALU.mult, g2_all), (ALU.add, beta2_all)):
+                    nc.gpsimd.tensor_tensor(
+                        out=z[:, half], in0=z[:, half], in1=rows[:, half], op=op
+                    )
+            return z
 
         for m in range(TOK_TILES):
             add_residual(m, 0)
+        spread_row("g2_psum", g2_rows)
+        spread_row("beta2_psum", beta2_rows)
         add_residual(0, 1)
+        add_residual(1, 1)
         statistics(0)
-        for m in range(TOK_TILES):
-            if m + 1 < TOK_TILES:
-                add_residual(m + 1, 1)
-                statistics(m + 1)
+        add_residual(2, 1)
+        statistics(1)
+        add_residual(3, 1)
+        z = normalise_without_vector(0)
+        statistics(2)
+        statistics(3)
+        for n in range(D_HALVES):
+            store(nc.scalar, 0, n, z)
+        for m in range(1, TOK_TILES):
             normalise(m)

@@ -26,6 +26,10 @@ D_HALVES = D // N_TILE
 W_BLOCKS = 2 * F_BLOCKS
 AHEAD = 7
 VECTOR_EXTRA_COLS = 160
+CHUNK = 256
+SCALAR_EXTRA_COLS = 64
+
+HALF_0_ADDS = {13: (0,), 14: (1,), 15: (2,)}
 
 FLOPS = 2 * TOK * D * F * 2
 
@@ -44,7 +48,7 @@ def tile_ffnn_encoder_pc_kernel(tc, h_attn, W1, b1, W2, b2, g2, beta2, out):
 
     with ExitStack() as ctx:
         keep = ctx.enter_context(tc.tile_pool(name="keep", bufs=1))
-        raw_pool = ctx.enter_context(tc.tile_pool(name="raw", bufs=AHEAD + 1))
+        raw_pool = ctx.enter_context(tc.tile_pool(name="raw", bufs=AHEAD))
         grouped_pool = ctx.enter_context(tc.tile_pool(name="grouped", bufs=6))
         codes_pool = ctx.enter_context(tc.tile_pool(name="codes", bufs=6))
         hid_pool = ctx.enter_context(tc.tile_pool(name="hid", bufs=3))
@@ -73,6 +77,9 @@ def tile_ffnn_encoder_pc_kernel(tc, h_attn, W1, b1, W2, b2, g2, beta2, out):
 
         raw = {}
 
+        def w2_piece(b, piece):
+            return divmod(2 * (b - F_BLOCKS) + piece, F_BLOCKS)
+
         def load_block(b):
             if b < F_BLOCKS:
                 rows = raw_pool.tile([P, D_PASSES, PACK, K_PASS], BF16, name="raw")
@@ -85,15 +92,33 @@ def tile_ffnn_encoder_pc_kernel(tc, h_attn, W1, b1, W2, b2, g2, beta2, out):
                     )
                 raw[b] = [rows[:, c] for c in range(D_PASSES)]
             else:
-                g = b - F_BLOCKS
-                rows = raw_pool.tile([P, PACK, D], BF16, name="raw")
-                nc.sync.dma_start(
-                    out=rows[:],
-                    in_=W2[g * K_PASS : (g + 1) * K_PASS, :].rearrange("(j p) x -> p j x", p=P),
-                )
-                raw[b] = [rows[:, :, n * N_TILE : (n + 1) * N_TILE] for n in range(D_HALVES)]
+                rows = raw_pool.tile([P, 2, PACK, N_TILE], BF16, name="raw")
+                for piece in range(2):
+                    n, g = w2_piece(b, piece)
+                    nc.sync.dma_start(
+                        out=rows[:, piece],
+                        in_=W2[
+                            g * K_PASS : (g + 1) * K_PASS, n * N_TILE : (n + 1) * N_TILE
+                        ].rearrange("(j p) x -> p j x", p=P),
+                    )
+                raw[b] = [rows[:, piece] for piece in range(2)]
 
-        load_block(0)
+        first_chunks = {}
+
+        def load_first_chunk(piece, part):
+            cols = slice(part * CHUNK, (part + 1) * CHUNK)
+            chunk = keep.tile([P, PACK, CHUNK], BF16, name="chunk%d%d" % (piece, part))
+            nc.sync.dma_start(
+                out=chunk[:],
+                in_=W1[piece * K_PASS : (piece + 1) * K_PASS, cols].rearrange(
+                    "(p j) x -> p j x", j=PACK
+                ),
+            )
+            first_chunks[(piece, part)] = chunk
+
+        for piece, part in ((0, 0), (1, 1), (0, 1), (1, 0)):
+            load_first_chunk(piece, part)
+        load_block(1)
         h_sb = keep.tile([P, TOK_TILES, D], BF16)
         h_view = h_rows.rearrange("(m p) d -> p m d", p=P)
         for pair in range(TOK_TILES // 2):
@@ -102,7 +127,7 @@ def tile_ffnn_encoder_pc_kernel(tc, h_attn, W1, b1, W2, b2, g2, beta2, out):
             )
         nc.sync.dma_start(out=b1_rows[0 : F // P, :], in_=b1.rearrange("(i p) -> i p", p=P))
         nc.sync.dma_start(out=b2_rows[0:1, :], in_=b2.rearrange("(o d) -> o d", o=1))
-        for b in range(1, AHEAD):
+        for b in range(2, AHEAD):
             load_block(b)
         nc.sync.dma_start(out=g2_rows[0:1, :], in_=g2.rearrange("(o d) -> o d", o=1))
         nc.sync.dma_start(out=beta2_rows[0:1, :], in_=beta2.rearrange("(o d) -> o d", o=1))
@@ -119,13 +144,33 @@ def tile_ffnn_encoder_pc_kernel(tc, h_attn, W1, b1, W2, b2, g2, beta2, out):
                 grouped[(b, piece)] = grouped_pool.tile(
                     [P, K_PASS, PACK], BF16, name="grouped", align_bytes=64
                 )
-            split = VECTOR_EXTRA_COLS if b < F_BLOCKS else 0
-            regroup(nc.vector.tensor_copy, grouped[(b, 0)][:], raw[b][0])
-            if split > 0:
-                regroup(
-                    nc.vector.tensor_copy, grouped[(b, 1)][:, :split, :], raw[b][1][:, :, :split]
-                )
-            regroup(nc.scalar.copy, grouped[(b, 1)][:, split:, :], raw[b][1][:, :, split:])
+            if b == 0:
+                for piece, part, engine_copy, first, last in (
+                    (0, 0, nc.vector.tensor_copy, 0, CHUNK),
+                    (1, 1, nc.scalar.copy, 0, CHUNK),
+                    (0, 1, nc.vector.tensor_copy, 0, CHUNK),
+                    (1, 0, nc.vector.tensor_copy, 0, VECTOR_EXTRA_COLS),
+                    (1, 0, nc.scalar.copy, VECTOR_EXTRA_COLS, CHUNK),
+                ):
+                    regroup(
+                        engine_copy,
+                        grouped[(b, piece)][:, part * CHUNK + first : part * CHUNK + last, :],
+                        first_chunks[(piece, part)][:, :, first:last],
+                    )
+                return
+            if b < F_BLOCKS:
+                ends = (K_PASS, VECTOR_EXTRA_COLS)
+            else:
+                ends = (K_PASS - SCALAR_EXTRA_COLS, 0)
+            for piece, end in enumerate(ends):
+                for engine_copy, first, last in (
+                    (nc.vector.tensor_copy, 0, end), (nc.scalar.copy, end, K_PASS)
+                ):
+                    if first < last:
+                        regroup(
+                            engine_copy, grouped[(b, piece)][:, first:last, :],
+                            raw[b][piece][:, :, first:last],
+                        )
 
         def quantise_piece(b, piece):
             codes = codes_pool.tile([P, K_PASS], U32, name="codes", align_bytes=64)
@@ -188,8 +233,9 @@ def tile_ffnn_encoder_pc_kernel(tc, h_attn, W1, b1, W2, b2, g2, beta2, out):
                 in_=hid_grouped[g][:].rearrange("p w j -> p (w j)"),
             )
 
-        def second_matmul(g, n):
-            codes, scales = packed[(F_BLOCKS + g, n)]
+        def second_matmul(b, piece):
+            n, g = w2_piece(b, piece)
+            codes, scales = packed[(b, piece)]
             for m in range(TOK_TILES):
                 if g == 0:
                     out_acc[(m, n)] = psum.tile([P, N_TILE], F32, name="out_acc", tag="bank")
@@ -256,35 +302,6 @@ def tile_ffnn_encoder_pc_kernel(tc, h_attn, W1, b1, W2, b2, g2, beta2, out):
             half = slice(n * N_TILE, (n + 1) * N_TILE)
             nc.scalar.copy(out=hb[:, m, half], in_=hb_acc[(m, n)][:])
 
-        for s in range(W_BLOCKS):
-            if s + AHEAD < W_BLOCKS:
-                load_block(s + AHEAD)
-            regroup_block(s)
-            if s >= 1:
-                quantise_piece(s - 1, 1)
-            if 0 <= s - 3 < F_BLOCKS:
-                regroup_hid(s - 3)
-            quantise_piece(s, 0)
-            if s == 0:
-                prepare_h()
-            if 0 <= s - 2 < F_BLOCKS:
-                relu_block(s - 2)
-            if 0 <= s - 1 < TOK_TILES * D_HALVES:
-                residual_copy(*divmod(s - 1, D_HALVES))
-            if 0 <= s - 1 < F_BLOCKS:
-                first_matmul(s - 1)
-            if s - 1 >= F_BLOCKS:
-                second_matmul(s - 1 - F_BLOCKS, 1)
-            if s >= F_BLOCKS:
-                second_matmul(s - F_BLOCKS, 0)
-            if 0 <= s - 3 < F_BLOCKS:
-                quantise_hid(s - 3)
-            if s < TOK_TILES * D_HALVES:
-                residual_matmul(*divmod(s, D_HALVES))
-
-        quantise_piece(W_BLOCKS - 1, 1)
-        second_matmul(F_BLOCKS - 1, 1)
-
         r = {}
         r_sum = {}
         neg_mean = {}
@@ -300,21 +317,88 @@ def tile_ffnn_encoder_pc_kernel(tc, h_attn, W1, b1, W2, b2, g2, beta2, out):
                 op0=ALU.mult, op1=ALU.add, accum_out=r_sum[m][:, n : n + 1],
             )
 
-        def statistics(m):
+        shift = {}
+        half_shift = {}
+        sq_sum = {}
+        var_0 = {}
+
+        def sum_squares(m, n):
+            if n == 0:
+                shift[m] = norm_pool.tile([P, 1], F32, name="shift")
+                half_shift[m] = norm_pool.tile([P, 1], F32, name="half_shift")
+                for column, factor in ((shift[m], -1.0 / N_TILE), (half_shift[m], -1.0 / D)):
+                    nc.scalar.activation(
+                        out=column[:], in_=r_sum[m][:, 0:1], func=ACT.Copy, scale=factor
+                    )
+                sq_sum[m] = norm_pool.tile([P, D_HALVES], F32, name="sq_sum")
+            half = slice(n * N_TILE, (n + 1) * N_TILE)
+            squares = norm_pool.tile([P, N_TILE], BF16, name="squares", bufs=2)
+            nc.scalar.activation(
+                out=squares[:], in_=r[m][:, half], func=ACT.Square, bias=shift[m][:], scale=1.0,
+                accum_out=sq_sum[m][:, n : n + 1],
+            )
+
+        for s in range(W_BLOCKS):
+            regroup_block(s)
+            if s + AHEAD < W_BLOCKS:
+                load_block(s + AHEAD)
+            if s >= 1:
+                quantise_piece(s - 1, 1)
+            if 0 <= s - 3 < F_BLOCKS:
+                regroup_hid(s - 3)
+            quantise_piece(s, 0)
+            if s == 1:
+                prepare_h()
+            if 0 <= s - 2 < F_BLOCKS:
+                relu_block(s - 2)
+            if 0 <= s - 2 < TOK_TILES * D_HALVES:
+                residual_copy(*divmod(s - 2, D_HALVES))
+            if 0 <= s - 1 < F_BLOCKS:
+                first_matmul(s - 1)
+            if 0 <= s - 1 < TOK_TILES * D_HALVES:
+                residual_matmul(*divmod(s - 1, D_HALVES))
+            if s - 1 >= F_BLOCKS:
+                second_matmul(s - 1, 1)
+            if s >= F_BLOCKS:
+                second_matmul(s, 0)
+            if 0 <= s - 3 < F_BLOCKS:
+                quantise_hid(s - 3)
+            for m in HALF_0_ADDS.get(s, ()):
+                add_residual(m, 0)
+            if s == W_BLOCKS - 1:
+                sum_squares(0, 0)
+                sum_squares(1, 0)
+
+        quantise_piece(W_BLOCKS - 1, 1)
+        second_matmul(W_BLOCKS - 1, 1)
+
+        def mean(m):
             neg_mean[m] = norm_pool.tile([P, 1], F32, name="neg_mean")
             nc.vector.tensor_scalar(
                 out=neg_mean[m][:], in0=r_sum[m][:, 0:1], scalar1=r_sum[m][:, 1:2],
                 scalar2=-1.0 / D, op0=ALU.add, op1=ALU.mult,
             )
-            squares = norm_pool.tile([P, D], BF16, name="squares", bufs=2)
-            sq_sum = norm_pool.tile([P, 1], F32, name="sq_sum")
+
+        def deviation(m):
+            gap_sq = norm_pool.tile([P, 1], F32, name="gap_sq")
             nc.scalar.activation(
-                out=squares[:], in_=r[m][:], func=ACT.Square, bias=neg_mean[m][:], scale=1.0,
-                accum_out=sq_sum[:],
+                out=gap_sq[:], in_=r_sum[m][:, 1:2], func=ACT.Square, bias=half_shift[m][:],
+                scale=1.0 / D,
+            )
+            var_0[m] = norm_pool.tile([P, 1], F32, name="var_0")
+            nc.scalar.activation(
+                out=var_0[m][:], in_=sq_sum[m][:, 0:1], func=ACT.Identity, bias=eps_col[:],
+                scale=1.0 / D,
+            )
+            sum_squares(m, 1)
+            offset = norm_pool.tile([P, 1], F32, name="offset")
+            nc.scalar.activation(
+                out=offset[:], in_=gap_sq[:], func=ACT.Identity, bias=var_0[m][:], scale=-1.0
             )
             std[m] = norm_pool.tile([P, 1], F32, name="std")
             nc.scalar.activation(
-                out=std[m][:], in_=sq_sum[:], func=ACT.Sqrt, bias=eps_col[:], scale=1.0 / D
+                out=std[m][:], in_=sq_sum[m][:, 1:2], func=ACT.Sqrt, bias=offset[:],
+                scale=1.0 / D,
             )
 
         norm_rows = {}
@@ -333,57 +417,108 @@ def tile_ffnn_encoder_pc_kernel(tc, h_attn, W1, b1, W2, b2, g2, beta2, out):
             half = slice(n * N_TILE, (n + 1) * N_TILE)
             queue.dma_start(out=out_rows[m * P : (m + 1) * P, half], in_=y[:, half])
 
-        def normalise(m):
-            y = norm_pool.tile([P, D], F32, name="y")
-            for n in range(D_HALVES):
-                half = slice(n * N_TILE, (n + 1) * N_TILE)
-                nc.vector.scalar_tensor_tensor(
-                    out=y[:, half], in0=r[m][:, half], scalar=neg_mean[m][:],
-                    in1=norm_rows["g2_psum"][n][:], op0=ALU.add, op1=ALU.mult,
-                )
-            rstd = norm_pool.tile([P, 1], F32, name="rstd")
-            nc.vector.reciprocal(out=rstd[:], in_=std[m][:])
-            for n in range(D_HALVES):
-                half = slice(n * N_TILE, (n + 1) * N_TILE)
-                nc.vector.scalar_tensor_tensor(
-                    out=y[:, half], in0=y[:, half], scalar=rstd[:],
-                    in1=norm_rows["beta2_psum"][n][:], op0=ALU.mult, op1=ALU.add,
-                )
-                store(nc.sync, m, n, y)
+        y = {}
+        rstd = {}
+        scale_diag = {}
+        scaled = {}
+
+        def weigh(m, n):
+            if n == 0:
+                y[m] = norm_pool.tile([P, D], F32, name="y")
+            half = slice(n * N_TILE, (n + 1) * N_TILE)
+            nc.vector.scalar_tensor_tensor(
+                out=y[m][:, half], in0=r[m][:, half], scalar=neg_mean[m][:],
+                in1=norm_rows["g2_psum"][n][:], op0=ALU.add, op1=ALU.mult,
+            )
+
+        def invert(m):
+            rstd[m] = norm_pool.tile([P, 1], F32, name="rstd")
+            nc.vector.reciprocal(out=rstd[m][:], in_=std[m][:])
+
+        def finish_by_vector(m, n):
+            half = slice(n * N_TILE, (n + 1) * N_TILE)
+            nc.vector.scalar_tensor_tensor(
+                out=y[m][:, half], in0=y[m][:, half], scalar=rstd[m][:],
+                in1=norm_rows["beta2_psum"][n][:], op0=ALU.mult, op1=ALU.add,
+            )
+            store(nc.sync, m, n, y[m])
+
+        def spread_scale(m):
+            scale_diag[m] = norm_pool.tile([P, P], F32, name="scale_diag", bufs=2)
+            nc.scalar.activation(
+                out=scale_diag[m][:], in_=ident_f32[:], func=ACT.Copy, scale=rstd[m][:]
+            )
+
+        def scale_by_tensor(m, n):
+            half = slice(n * N_TILE, (n + 1) * N_TILE)
+            scaled[(m, n)] = psum.tile([P, N_TILE], F32, name="scaled", tag="bank")
+            nc.tensor.matmul(
+                out=scaled[(m, n)][:], lhsT=ones_bf16[:], rhs=beta2_rows[:, half],
+                start=True, stop=False,
+            )
+            nc.tensor.matmul(
+                out=scaled[(m, n)][:], lhsT=scale_diag[m][:], rhs=y[m][:, half],
+                start=False, stop=True,
+            )
+
+        def empty_scaled(m, n):
+            half = slice(n * N_TILE, (n + 1) * N_TILE)
+            done = norm_pool.tile([P, N_TILE], F32, name="done", bufs=3)
+            nc.scalar.copy(out=done[:], in_=scaled[(m, n)][:])
+            nc.scalar.dma_start(out=out_rows[m * P : (m + 1) * P, half], in_=done[:])
 
         def normalise_without_vector(m):
-            rstd = norm_pool.tile([P, 1], F32, name="rstd")
-            nc.vector.reciprocal(out=rstd[:], in_=std[m][:])
-            shift = norm_pool.tile([P, 1], F32, name="shift", bufs=1)
+            z_bias = norm_pool.tile([P, 1], F32, name="z_bias", bufs=1)
             nc.vector.tensor_scalar(
-                out=shift[:], in0=neg_mean[m][:], scalar1=rstd[:], scalar2=None, op0=ALU.mult
+                out=z_bias[:], in0=neg_mean[m][:], scalar1=rstd[m][:], scalar2=None, op0=ALU.mult
             )
             z = norm_pool.tile([P, D], F32, name="y")
-            nc.scalar.activation(
-                out=z[:], in_=r[m][:], func=ACT.Identity, bias=shift[:], scale=rstd[:]
-            )
             for n in range(D_HALVES):
                 half = slice(n * N_TILE, (n + 1) * N_TILE)
+                nc.scalar.activation(
+                    out=z[:, half], in_=r[m][:, half], func=ACT.Identity, bias=z_bias[:],
+                    scale=rstd[m][:],
+                )
                 for op, rows in ((ALU.mult, g2_all), (ALU.add, beta2_all)):
                     nc.gpsimd.tensor_tensor(
                         out=z[:, half], in0=z[:, half], in1=rows[:, half], op=op
                     )
             return z
 
-        for m in range(TOK_TILES):
-            add_residual(m, 0)
+        for m in range(2, TOK_TILES - 1):
+            sum_squares(m, 0)
+        add_residual(3, 0)
+        sum_squares(3, 0)
         spread_row("g2_psum", g2_rows)
         spread_row("beta2_psum", beta2_rows)
-        add_residual(0, 1)
-        add_residual(1, 1)
-        statistics(0)
-        add_residual(2, 1)
-        statistics(1)
-        add_residual(3, 1)
+        for m in range(TOK_TILES):
+            add_residual(m, 1)
+            if m >= 1:
+                mean(m - 1)
+            if m < 2:
+                deviation(m)
+        invert(0)
+        mean(3)
         z = normalise_without_vector(0)
-        statistics(2)
-        statistics(3)
-        for n in range(D_HALVES):
-            store(nc.scalar, 0, n, z)
-        for m in range(1, TOK_TILES):
-            normalise(m)
+        weigh(1, 0)
+        invert(1)
+        weigh(1, 1)
+        spread_scale(1)
+        deviation(2)
+        deviation(3)
+        scale_by_tensor(1, 0)
+        scale_by_tensor(1, 1)
+        weigh(2, 0)
+        weigh(2, 1)
+        invert(2)
+        weigh(3, 0)
+        empty_scaled(1, 0)
+        finish_by_vector(2, 0)
+        finish_by_vector(2, 1)
+        invert(3)
+        weigh(3, 1)
+        empty_scaled(1, 1)
+        store(nc.sync, 0, 0, z)
+        finish_by_vector(3, 0)
+        finish_by_vector(3, 1)
+        store(nc.scalar, 0, 1, z)

@@ -26,8 +26,8 @@ D_HALVES = D // N_TILE
 W_BLOCKS = 2 * F_BLOCKS
 AHEAD = 7
 VECTOR_EXTRA_COLS = 160
-CHUNK = 256
-SCALAR_EXTRA_COLS = 64
+VECTOR_COLS_START = 336
+SCALAR_EXTRA_COLS = 48
 
 HALF_0_ADDS = {13: (0,), 14: (1,), 15: (2,)}
 
@@ -80,51 +80,37 @@ def tile_ffnn_encoder_pc_kernel(tc, h_attn, W1, b1, W2, b2, g2, beta2, out):
         def w2_piece(b, piece):
             return divmod(2 * (b - F_BLOCKS) + piece, F_BLOCKS)
 
-        def load_block(b):
+        def load_piece(b, piece):
+            if piece == 0:
+                raw[b] = raw_pool.tile([P, 2, PACK, K_PASS], BF16, name="raw")
             if b < F_BLOCKS:
-                rows = raw_pool.tile([P, D_PASSES, PACK, K_PASS], BF16, name="raw")
-                for c in range(D_PASSES):
-                    nc.sync.dma_start(
-                        out=rows[:, c],
-                        in_=W1[
-                            c * K_PASS : (c + 1) * K_PASS, b * K_PASS : (b + 1) * K_PASS
-                        ].rearrange("(p j) x -> p j x", j=PACK),
-                    )
-                raw[b] = [rows[:, c] for c in range(D_PASSES)]
+                source = W1[
+                    piece * K_PASS : (piece + 1) * K_PASS, b * K_PASS : (b + 1) * K_PASS
+                ].rearrange("(p j) x -> p j x", j=PACK)
             else:
-                rows = raw_pool.tile([P, 2, PACK, N_TILE], BF16, name="raw")
-                for piece in range(2):
-                    n, g = w2_piece(b, piece)
-                    nc.sync.dma_start(
-                        out=rows[:, piece],
-                        in_=W2[
-                            g * K_PASS : (g + 1) * K_PASS, n * N_TILE : (n + 1) * N_TILE
-                        ].rearrange("(j p) x -> p j x", p=P),
-                    )
-                raw[b] = [rows[:, piece] for piece in range(2)]
+                n, g = w2_piece(b, piece)
+                source = W2[
+                    g * K_PASS : (g + 1) * K_PASS, n * N_TILE : (n + 1) * N_TILE
+                ].rearrange("(j p) x -> p j x", p=P)
+            nc.sync.dma_start(out=raw[b][:, piece], in_=source)
 
-        first_chunks = {}
+        def load_block(b):
+            load_piece(b, 0)
+            load_piece(b, 1)
 
-        def load_first_chunk(piece, part):
-            cols = slice(part * CHUNK, (part + 1) * CHUNK)
-            chunk = keep.tile([P, PACK, CHUNK], BF16, name="chunk%d%d" % (piece, part))
-            nc.sync.dma_start(
-                out=chunk[:],
-                in_=W1[piece * K_PASS : (piece + 1) * K_PASS, cols].rearrange(
-                    "(p j) x -> p j x", j=PACK
-                ),
-            )
-            first_chunks[(piece, part)] = chunk
-
-        for piece, part in ((0, 0), (1, 1), (0, 1), (1, 0)):
-            load_first_chunk(piece, part)
-        load_block(1)
         h_sb = keep.tile([P, TOK_TILES, D], BF16)
         h_view = h_rows.rearrange("(m p) d -> p m d", p=P)
-        for pair in range(TOK_TILES // 2):
-            nc.sync.dma_start(
-                out=h_sb[:, 2 * pair : 2 * pair + 2, :], in_=h_view[:, 2 * pair : 2 * pair + 2, :]
-            )
+
+        def load_h(pair):
+            tiles = slice(2 * pair, 2 * pair + 2)
+            nc.sync.dma_start(out=h_sb[:, tiles, :], in_=h_view[:, tiles, :])
+
+        load_piece(0, 0)
+        load_piece(0, 1)
+        load_h(0)
+        load_piece(1, 0)
+        load_h(1)
+        load_piece(1, 1)
         nc.sync.dma_start(out=b1_rows[0 : F // P, :], in_=b1.rearrange("(i p) -> i p", p=P))
         nc.sync.dma_start(out=b2_rows[0:1, :], in_=b2.rearrange("(o d) -> o d", o=1))
         for b in range(2, AHEAD):
@@ -139,38 +125,30 @@ def tile_ffnn_encoder_pc_kernel(tc, h_attn, W1, b1, W2, b2, g2, beta2, out):
         grouped = {}
         packed = {}
 
-        def regroup_block(b):
+        def new_grouped(b):
             for piece in range(2):
                 grouped[(b, piece)] = grouped_pool.tile(
                     [P, K_PASS, PACK], BF16, name="grouped", align_bytes=64
                 )
-            if b == 0:
-                for piece, part, engine_copy, first, last in (
-                    (0, 0, nc.vector.tensor_copy, 0, CHUNK),
-                    (1, 1, nc.scalar.copy, 0, CHUNK),
-                    (0, 1, nc.vector.tensor_copy, 0, CHUNK),
-                    (1, 0, nc.vector.tensor_copy, 0, VECTOR_EXTRA_COLS),
-                    (1, 0, nc.scalar.copy, VECTOR_EXTRA_COLS, CHUNK),
-                ):
+
+        def regroup_piece(b, piece, split):
+            for engine_copy, first, last in (
+                (nc.vector.tensor_copy, 0, split), (nc.scalar.copy, split, K_PASS)
+            ):
+                if first < last:
                     regroup(
-                        engine_copy,
-                        grouped[(b, piece)][:, part * CHUNK + first : part * CHUNK + last, :],
-                        first_chunks[(piece, part)][:, :, first:last],
+                        engine_copy, grouped[(b, piece)][:, first:last, :],
+                        raw[b][:, piece, :, first:last],
                     )
-                return
+
+        def regroup_block(b):
+            new_grouped(b)
             if b < F_BLOCKS:
-                ends = (K_PASS, VECTOR_EXTRA_COLS)
+                splits = (K_PASS, VECTOR_EXTRA_COLS)
             else:
-                ends = (K_PASS - SCALAR_EXTRA_COLS, 0)
-            for piece, end in enumerate(ends):
-                for engine_copy, first, last in (
-                    (nc.vector.tensor_copy, 0, end), (nc.scalar.copy, end, K_PASS)
-                ):
-                    if first < last:
-                        regroup(
-                            engine_copy, grouped[(b, piece)][:, first:last, :],
-                            raw[b][piece][:, :, first:last],
-                        )
+                splits = (K_PASS - SCALAR_EXTRA_COLS, 0)
+            for piece in range(2):
+                regroup_piece(b, piece, splits[piece])
 
         def quantise_piece(b, piece):
             codes = codes_pool.tile([P, K_PASS], U32, name="codes", align_bytes=64)
@@ -250,38 +228,41 @@ def tile_ffnn_encoder_pc_kernel(tc, h_attn, W1, b1, W2, b2, g2, beta2, out):
                     stop=(g == F_BLOCKS - 1),
                 )
 
-        def prepare_h():
+        def regroup_h(pair):
             words_per_pass = K_PASS // 2
-            for pair in range(TOK_TILES // 2):
-                for c in range(D_PASSES):
-                    xt = psum.tile([P, 2, 2, P], F32, name="xt", tag="bank")
-                    for mm in range(2):
-                        h_words = h_sb[:, 2 * pair + mm, :].bitcast(F32)
-                        for u in range(2):
-                            nc.tensor.transpose(
-                                xt[:, mm, u, :],
-                                h_words[:, c * words_per_pass + u : (c + 1) * words_per_pass : 2],
-                                ident_f32[:],
-                            )
-                    dst = (
-                        h_grouped[:, c, pair * 2 * P * PACK : (pair + 1) * 2 * P * PACK]
-                        .bitcast(F32)
-                        .rearrange("p (m k u) -> p m k u", m=2, u=2)
-                    )
-                    src = xt[:].rearrange("p m u k -> p m k u")
-                    if c == 0:
-                        nc.vector.tensor_copy(out=dst, in_=src)
-                    else:
-                        nc.scalar.copy(out=dst, in_=src)
-            b1_t = psum.tile([P, P], BF16, name="b1_t", tag="bank")
-            nc.tensor.transpose(b1_t[:], b1_rows[:], ident_bf16[:])
-            nc.vector.tensor_copy(out=b1_cols[:], in_=b1_t[:, 0 : F // P])
+            for c in range(D_PASSES):
+                xt = psum.tile([P, 2, 2, P], F32, name="xt", tag="bank")
+                for mm in range(2):
+                    h_words = h_sb[:, 2 * pair + mm, :].bitcast(F32)
+                    for u in range(2):
+                        nc.tensor.transpose(
+                            xt[:, mm, u, :],
+                            h_words[:, c * words_per_pass + u : (c + 1) * words_per_pass : 2],
+                            ident_f32[:],
+                        )
+                dst = (
+                    h_grouped[:, c, pair * 2 * P * PACK : (pair + 1) * 2 * P * PACK]
+                    .bitcast(F32)
+                    .rearrange("p (m k u) -> p m k u", m=2, u=2)
+                )
+                src = xt[:].rearrange("p m u k -> p m k u")
+                if c == 0:
+                    nc.vector.tensor_copy(out=dst, in_=src)
+                else:
+                    nc.scalar.copy(out=dst, in_=src)
+
+        def quantise_h():
             for c in range(D_PASSES):
                 nc.vector.quantize_mx(
                     out=h_codes[:, c, :].bitcast(FP8X4),
                     scales=h_scales[:, c, :],
                     in_=h_grouped[:, c, :],
                 )
+
+        def spread_b1():
+            b1_t = psum.tile([P, P], BF16, name="b1_t", tag="bank")
+            nc.tensor.transpose(b1_t[:], b1_rows[:], ident_bf16[:])
+            nc.vector.tensor_copy(out=b1_cols[:], in_=b1_t[:, 0 : F // P])
 
         hb = keep.tile([P, TOK_TILES, D], F32)
         hb_acc = {}
@@ -338,17 +319,30 @@ def tile_ffnn_encoder_pc_kernel(tc, h_attn, W1, b1, W2, b2, g2, beta2, out):
                 accum_out=sq_sum[m][:, n : n + 1],
             )
 
-        for s in range(W_BLOCKS):
+        new_grouped(0)
+        new_grouped(1)
+        regroup_piece(0, 0, VECTOR_COLS_START)
+        regroup_piece(0, 1, VECTOR_COLS_START)
+        quantise_piece(0, 0)
+        regroup_h(0)
+        quantise_piece(0, 1)
+        regroup_piece(1, 0, VECTOR_COLS_START)
+        regroup_h(1)
+        spread_b1()
+        quantise_h()
+        regroup_piece(1, 1, VECTOR_COLS_START)
+        quantise_piece(1, 0)
+        load_block(AHEAD)
+        first_matmul(0)
+        residual_matmul(0, 0)
+        for s in range(2, W_BLOCKS):
             regroup_block(s)
-            if s + AHEAD < W_BLOCKS:
-                load_block(s + AHEAD)
-            if s >= 1:
-                quantise_piece(s - 1, 1)
+            if s + AHEAD - 1 < W_BLOCKS:
+                load_block(s + AHEAD - 1)
+            quantise_piece(s - 1, 1)
             if 0 <= s - 3 < F_BLOCKS:
                 regroup_hid(s - 3)
             quantise_piece(s, 0)
-            if s == 1:
-                prepare_h()
             if 0 <= s - 2 < F_BLOCKS:
                 relu_block(s - 2)
             if 0 <= s - 2 < TOK_TILES * D_HALVES:
@@ -419,8 +413,6 @@ def tile_ffnn_encoder_pc_kernel(tc, h_attn, W1, b1, W2, b2, g2, beta2, out):
 
         y = {}
         rstd = {}
-        scale_diag = {}
-        scaled = {}
 
         def weigh(m, n):
             if n == 0:
@@ -442,30 +434,6 @@ def tile_ffnn_encoder_pc_kernel(tc, h_attn, W1, b1, W2, b2, g2, beta2, out):
                 in1=norm_rows["beta2_psum"][n][:], op0=ALU.mult, op1=ALU.add,
             )
             store(nc.sync, m, n, y[m])
-
-        def spread_scale(m):
-            scale_diag[m] = norm_pool.tile([P, P], F32, name="scale_diag", bufs=2)
-            nc.scalar.activation(
-                out=scale_diag[m][:], in_=ident_f32[:], func=ACT.Copy, scale=rstd[m][:]
-            )
-
-        def scale_by_tensor(m, n):
-            half = slice(n * N_TILE, (n + 1) * N_TILE)
-            scaled[(m, n)] = psum.tile([P, N_TILE], F32, name="scaled", tag="bank")
-            nc.tensor.matmul(
-                out=scaled[(m, n)][:], lhsT=ones_bf16[:], rhs=beta2_rows[:, half],
-                start=True, stop=False,
-            )
-            nc.tensor.matmul(
-                out=scaled[(m, n)][:], lhsT=scale_diag[m][:], rhs=y[m][:, half],
-                start=False, stop=True,
-            )
-
-        def empty_scaled(m, n):
-            half = slice(n * N_TILE, (n + 1) * N_TILE)
-            done = norm_pool.tile([P, N_TILE], F32, name="done", bufs=3)
-            nc.scalar.copy(out=done[:], in_=scaled[(m, n)][:])
-            nc.scalar.dma_start(out=out_rows[m * P : (m + 1) * P, half], in_=done[:])
 
         def normalise_without_vector(m):
             z_bias = norm_pool.tile([P, 1], F32, name="z_bias", bufs=1)
@@ -503,22 +471,19 @@ def tile_ffnn_encoder_pc_kernel(tc, h_attn, W1, b1, W2, b2, g2, beta2, out):
         weigh(1, 0)
         invert(1)
         weigh(1, 1)
-        spread_scale(1)
         deviation(2)
         deviation(3)
-        scale_by_tensor(1, 0)
-        scale_by_tensor(1, 1)
+        finish_by_vector(1, 0)
+        finish_by_vector(1, 1)
         weigh(2, 0)
         weigh(2, 1)
         invert(2)
         weigh(3, 0)
-        empty_scaled(1, 0)
+        weigh(3, 1)
+        invert(3)
         finish_by_vector(2, 0)
         finish_by_vector(2, 1)
-        invert(3)
-        weigh(3, 1)
-        empty_scaled(1, 1)
-        store(nc.sync, 0, 0, z)
+        store(nc.scalar, 0, 0, z)
         finish_by_vector(3, 0)
         finish_by_vector(3, 1)
         store(nc.scalar, 0, 1, z)

@@ -25,7 +25,8 @@ F_BLOCKS = F // K_PASS
 D_HALVES = D // N_TILE
 W_BLOCKS = 2 * F_BLOCKS
 AHEAD = 7
-VECTOR_EXTRA_COLS = 160
+VECTOR_EXTRA_COLS = 64
+MOVED_COLS = 256
 VECTOR_COLS_START = 336
 SCALAR_EXTRA_COLS = 48
 
@@ -131,9 +132,9 @@ def tile_ffnn_encoder_pc_kernel(tc, h_attn, W1, b1, W2, b2, g2, beta2, out):
                     [P, K_PASS, PACK], BF16, name="grouped", align_bytes=64
                 )
 
-        def regroup_piece(b, piece, split):
+        def regroup_piece(b, piece, split, end=K_PASS):
             for engine_copy, first, last in (
-                (nc.vector.tensor_copy, 0, split), (nc.scalar.copy, split, K_PASS)
+                (nc.vector.tensor_copy, 0, split), (nc.scalar.copy, split, end)
             ):
                 if first < last:
                     regroup(
@@ -147,8 +148,26 @@ def tile_ffnn_encoder_pc_kernel(tc, h_attn, W1, b1, W2, b2, g2, beta2, out):
                 splits = (K_PASS, VECTOR_EXTRA_COLS)
             else:
                 splits = (K_PASS - SCALAR_EXTRA_COLS, 0)
+            if b in moved:
+                regroup_piece(b, 0, K_PASS)
+                regroup_piece(b, 1, VECTOR_EXTRA_COLS, K_PASS - MOVED_COLS)
+                nc.scalar.copy(
+                    out=grouped[(b, 1)][:, K_PASS - MOVED_COLS :, :],
+                    in_=moved[b][:].rearrange("p j w -> p w j"),
+                )
+                return
             for piece in range(2):
                 regroup_piece(b, piece, splits[piece])
+
+        moved = {}
+
+        def move_columns(b):
+            moved[b] = psum.tile([P, PACK, MOVED_COLS], BF16, name="moved", tag="bank")
+            for j in range(PACK):
+                nc.tensor.matmul(
+                    out=moved[b][:, j, :], lhsT=ident_bf16[:],
+                    rhs=raw[b][:, 1, j, K_PASS - MOVED_COLS :], start=True, stop=True,
+                )
 
         def quantise_piece(b, piece):
             codes = codes_pool.tile([P, K_PASS], U32, name="codes", align_bytes=64)
@@ -333,6 +352,7 @@ def tile_ffnn_encoder_pc_kernel(tc, h_attn, W1, b1, W2, b2, g2, beta2, out):
         regroup_piece(1, 1, VECTOR_COLS_START)
         quantise_piece(1, 0)
         load_block(AHEAD)
+        move_columns(2)
         first_matmul(0)
         residual_matmul(0, 0)
         for s in range(2, W_BLOCKS):
@@ -347,6 +367,8 @@ def tile_ffnn_encoder_pc_kernel(tc, h_attn, W1, b1, W2, b2, g2, beta2, out):
                 relu_block(s - 2)
             if 0 <= s - 2 < TOK_TILES * D_HALVES:
                 residual_copy(*divmod(s - 2, D_HALVES))
+            if s + 1 < F_BLOCKS:
+                move_columns(s + 1)
             if 0 <= s - 1 < F_BLOCKS:
                 first_matmul(s - 1)
             if 0 <= s - 1 < TOK_TILES * D_HALVES:

@@ -25,7 +25,7 @@ F_BLOCKS = F // K_PASS
 D_HALVES = D // N_TILE
 W_BLOCKS = 2 * F_BLOCKS
 AHEAD = 7
-VECTOR_EXTRA_COLS = 64
+VECTOR_EXTRA_COLS = 96
 MOVED_COLS = 256
 VECTOR_COLS_START = 336
 SCALAR_EXTRA_COLS = 48
@@ -66,15 +66,12 @@ def tile_ffnn_encoder_pc_kernel(tc, h_attn, W1, b1, W2, b2, g2, beta2, out):
         ident_bf16 = keep.tile([P, P], BF16)
         make_identity(nc, ident_bf16[:])
         b1_rows = keep.tile([P, P], BF16)
-        nc.vector.memset(b1_rows[:], 0.0)
-        ones_bf16 = keep.tile([P, P], BF16)
-        nc.vector.memset(ones_bf16[:], 1.0)
+        nc.gpsimd.memset(b1_rows[:], 0.0)
+        row_0 = keep.tile([P, P], BF16)
+        nc.vector.memset(row_0[:], 0.0)
+        nc.vector.memset(row_0[0:1, :], 1.0)
         b2_rows = keep.tile([P, D], BF16)
-        nc.vector.memset(b2_rows[:], 0.0)
-        g2_rows = keep.tile([P, D], BF16)
-        nc.vector.memset(g2_rows[:], 0.0)
-        beta2_rows = keep.tile([P, D], BF16)
-        nc.vector.memset(beta2_rows[:], 0.0)
+        nc.gpsimd.memset(b2_rows[:], 0.0)
 
         raw = {}
 
@@ -116,8 +113,6 @@ def tile_ffnn_encoder_pc_kernel(tc, h_attn, W1, b1, W2, b2, g2, beta2, out):
         nc.sync.dma_start(out=b2_rows[0:1, :], in_=b2.rearrange("(o d) -> o d", o=1))
         for b in range(2, AHEAD):
             load_block(b)
-        nc.sync.dma_start(out=g2_rows[0:1, :], in_=g2.rearrange("(o d) -> o d", o=1))
-        nc.sync.dma_start(out=beta2_rows[0:1, :], in_=beta2.rearrange("(o d) -> o d", o=1))
         g2_all = keep.tile([P, D], BF16)
         nc.sync.dma_start(out=g2_all[:], in_=g2.partition_broadcast(P))
         beta2_all = keep.tile([P, D], BF16)
@@ -153,7 +148,7 @@ def tile_ffnn_encoder_pc_kernel(tc, h_attn, W1, b1, W2, b2, g2, beta2, out):
                 regroup_piece(b, 1, VECTOR_EXTRA_COLS, K_PASS - MOVED_COLS)
                 nc.scalar.copy(
                     out=grouped[(b, 1)][:, K_PASS - MOVED_COLS :, :],
-                    in_=moved[b][:].rearrange("p j w -> p w j"),
+                    in_=moved[b][:],
                 )
                 return
             for piece in range(2):
@@ -162,11 +157,13 @@ def tile_ffnn_encoder_pc_kernel(tc, h_attn, W1, b1, W2, b2, g2, beta2, out):
         moved = {}
 
         def move_columns(b):
-            moved[b] = psum.tile([P, PACK, MOVED_COLS], BF16, name="moved", tag="bank")
-            for j in range(PACK):
+            moved[b] = psum.tile([P, MOVED_COLS, PACK], BF16, name="moved", tag="bank")
+            for k in range(0, MOVED_COLS, P):
+                first = K_PASS - MOVED_COLS + k
                 nc.tensor.matmul(
-                    out=moved[b][:, j, :], lhsT=ident_bf16[:],
-                    rhs=raw[b][:, 1, j, K_PASS - MOVED_COLS :], start=True, stop=True,
+                    out=moved[b][:, k : k + P, :].rearrange("p w j -> p j w"),
+                    lhsT=ident_bf16[:], rhs=raw[b][:, 1, :, first : first + P],
+                    start=True, stop=True,
                 )
 
         def quantise_piece(b, piece):
@@ -294,7 +291,7 @@ def tile_ffnn_encoder_pc_kernel(tc, h_attn, W1, b1, W2, b2, g2, beta2, out):
                 start=True, stop=False,
             )
             nc.tensor.matmul(
-                out=hb_acc[(m, n)][:], lhsT=ones_bf16[:], rhs=b2_rows[:, half],
+                out=hb_acc[(m, n)][:], lhsT=row_0[:], rhs=b2_rows[:, half],
                 start=False, stop=True,
             )
 
@@ -424,7 +421,7 @@ def tile_ffnn_encoder_pc_kernel(tc, h_attn, W1, b1, W2, b2, g2, beta2, out):
             for n in range(D_HALVES):
                 bank = psum.tile([P, N_TILE], F32, name=name, tag="bank")
                 nc.tensor.matmul(
-                    out=bank[:], lhsT=ones_bf16[:], rhs=rows[:, n * N_TILE : (n + 1) * N_TILE],
+                    out=bank[:], lhsT=row_0[:], rhs=rows[:, n * N_TILE : (n + 1) * N_TILE],
                     start=True, stop=True,
                 )
                 norm_rows[name].append(bank)
@@ -479,8 +476,8 @@ def tile_ffnn_encoder_pc_kernel(tc, h_attn, W1, b1, W2, b2, g2, beta2, out):
             sum_squares(m, 0)
         add_residual(3, 0)
         sum_squares(3, 0)
-        spread_row("g2_psum", g2_rows)
-        spread_row("beta2_psum", beta2_rows)
+        spread_row("g2_psum", g2_all)
+        spread_row("beta2_psum", beta2_all)
         for m in range(TOK_TILES):
             add_residual(m, 1)
             if m >= 1:

@@ -25,10 +25,10 @@ F_BLOCKS = F // K_PASS
 D_HALVES = D // N_TILE
 W_BLOCKS = 2 * F_BLOCKS
 AHEAD = 7
-VECTOR_EXTRA_COLS = 96
+VECTOR_EXTRA_COLS = 64
 MOVED_COLS = 256
 VECTOR_COLS_START = 336
-SCALAR_EXTRA_COLS = 48
+SCALAR_EXTRA_COLS = 64
 
 HALF_0_ADDS = {13: (0,), 14: (1,), 15: (2,)}
 
@@ -66,12 +66,12 @@ def tile_ffnn_encoder_pc_kernel(tc, h_attn, W1, b1, W2, b2, g2, beta2, out):
         ident_bf16 = keep.tile([P, P], BF16)
         make_identity(nc, ident_bf16[:])
         b1_rows = keep.tile([P, P], BF16)
-        nc.gpsimd.memset(b1_rows[:], 0.0)
+        nc.vector.memset(b1_rows[:], 0.0)
         row_0 = keep.tile([P, P], BF16)
         nc.vector.memset(row_0[:], 0.0)
         nc.vector.memset(row_0[0:1, :], 1.0)
         b2_rows = keep.tile([P, D], BF16)
-        nc.gpsimd.memset(b2_rows[:], 0.0)
+        nc.vector.memset(b2_rows[:], 0.0)
 
         raw = {}
 
@@ -106,11 +106,11 @@ def tile_ffnn_encoder_pc_kernel(tc, h_attn, W1, b1, W2, b2, g2, beta2, out):
         load_piece(0, 0)
         load_piece(0, 1)
         load_h(0)
+        nc.sync.dma_start(out=b2_rows[0:1, :], in_=b2.rearrange("(o d) -> o d", o=1))
         load_piece(1, 0)
         load_h(1)
         load_piece(1, 1)
         nc.sync.dma_start(out=b1_rows[0 : F // P, :], in_=b1.rearrange("(i p) -> i p", p=P))
-        nc.sync.dma_start(out=b2_rows[0:1, :], in_=b2.rearrange("(o d) -> o d", o=1))
         for b in range(2, AHEAD):
             load_block(b)
         g2_all = keep.tile([P, D], BF16)
@@ -146,13 +146,14 @@ def tile_ffnn_encoder_pc_kernel(tc, h_attn, W1, b1, W2, b2, g2, beta2, out):
             if b in moved:
                 regroup_piece(b, 0, K_PASS)
                 regroup_piece(b, 1, VECTOR_EXTRA_COLS, K_PASS - MOVED_COLS)
-                nc.scalar.copy(
-                    out=grouped[(b, 1)][:, K_PASS - MOVED_COLS :, :],
-                    in_=moved[b][:],
-                )
                 return
             for piece in range(2):
                 regroup_piece(b, piece, splits[piece])
+
+        def take_moved(b):
+            nc.scalar.copy(
+                out=grouped[(b, 1)][:, K_PASS - MOVED_COLS :, :], in_=moved[b][:]
+            )
 
         moved = {}
 
@@ -341,17 +342,26 @@ def tile_ffnn_encoder_pc_kernel(tc, h_attn, W1, b1, W2, b2, g2, beta2, out):
         regroup_piece(0, 1, VECTOR_COLS_START)
         quantise_piece(0, 0)
         regroup_h(0)
+        for n in range(D_HALVES):
+            residual_matmul(0, n)
         quantise_piece(0, 1)
+        for n in range(D_HALVES):
+            residual_copy(0, n)
         regroup_piece(1, 0, VECTOR_COLS_START)
         regroup_h(1)
         spread_b1()
+        for n in range(D_HALVES):
+            residual_matmul(1, n)
         quantise_h()
         regroup_piece(1, 1, VECTOR_COLS_START)
+        for n in range(D_HALVES):
+            residual_copy(1, n)
         quantise_piece(1, 0)
         load_block(AHEAD)
-        move_columns(2)
         first_matmul(0)
-        residual_matmul(0, 0)
+        move_columns(2)
+        later = [(m, n) for m in (2, 3) for n in range(D_HALVES)]
+        residual_matmul(*later[0])
         for s in range(2, W_BLOCKS):
             regroup_block(s)
             if s + AHEAD - 1 < W_BLOCKS:
@@ -362,14 +372,16 @@ def tile_ffnn_encoder_pc_kernel(tc, h_attn, W1, b1, W2, b2, g2, beta2, out):
             quantise_piece(s, 0)
             if 0 <= s - 2 < F_BLOCKS:
                 relu_block(s - 2)
-            if 0 <= s - 2 < TOK_TILES * D_HALVES:
-                residual_copy(*divmod(s - 2, D_HALVES))
+            if s in moved:
+                take_moved(s)
+            if s - 2 < len(later):
+                residual_copy(*later[s - 2])
             if s + 1 < F_BLOCKS:
                 move_columns(s + 1)
             if 0 <= s - 1 < F_BLOCKS:
                 first_matmul(s - 1)
-            if 0 <= s - 1 < TOK_TILES * D_HALVES:
-                residual_matmul(*divmod(s - 1, D_HALVES))
+            if s - 1 < len(later):
+                residual_matmul(*later[s - 1])
             if s - 1 >= F_BLOCKS:
                 second_matmul(s - 1, 1)
             if s >= F_BLOCKS:

from contextlib import ExitStack

import concourse.mybir as mybir
from concourse.masks import make_identity

F32 = mybir.dt.float32
BF16 = mybir.dt.bfloat16
U32 = mybir.dt.uint32
U8 = mybir.dt.uint8
FP8X4 = mybir.dt.float8_e4m3fn_x4
ACT = mybir.ActivationFunctionType
ALU = mybir.AluOpType

P = 128
PACK = 4
K_PASS = P * PACK
TOK = 512
D = 1024
F = 4096
EPS = 1e-3
N_TILE = 512
TOK_TILES = TOK // P
D_PASSES = D // K_PASS
F_BLOCKS = F // K_PASS
D_HALVES = D // N_TILE
W_BLOCKS = 2 * F_BLOCKS
AHEAD = 7
VECTOR_EXTRA_COLS = 64
MOVED_COLS = 256
VECTOR_COLS_START = 336
SCALAR_EXTRA_COLS = 64

HALF_0_ADDS = {13: (0,), 14: (1,), 15: (2,)}

FLOPS = 2 * TOK * D * F * 2


def regroup(engine_copy, grouped, rows):
    engine_copy(
        out=grouped.rearrange("p (c i) j -> p c j i", i=8),
        in_=rows.rearrange("p j (c i) -> p c j i", i=8),
    )


def tile_ffnn_encoder_pc_kernel(tc, h_attn, W1, b1, W2, b2, g2, beta2, out):
    nc = tc.nc
    h_rows = h_attn.rearrange("b s d -> (b s) d")
    out_rows = out.rearrange("b s d -> (b s) d")

    with ExitStack() as ctx:
        keep = ctx.enter_context(tc.tile_pool(name="keep", bufs=1))
        raw_pool = ctx.enter_context(tc.tile_pool(name="raw", bufs=AHEAD))
        grouped_pool = ctx.enter_context(tc.tile_pool(name="grouped", bufs=6))
        codes_pool = ctx.enter_context(tc.tile_pool(name="codes", bufs=6))
        hid_pool = ctx.enter_context(tc.tile_pool(name="hid", bufs=3))
        norm_pool = ctx.enter_context(tc.tile_pool(name="norm", bufs=4))
        psum = ctx.enter_context(tc.psum_pool(name="psum", bufs=8))
        ctx.enter_context(tc.manual_schedule())

        eps_col = keep.tile([P, 1], F32)
        nc.vector.memset(eps_col[:], EPS)
        warm_col = keep.tile([P, 1], F32)
        nc.scalar.activation(out=warm_col[:], in_=eps_col[:], func=ACT.Sqrt)
        ident_f32 = keep.tile([P, P], F32)
        make_identity(nc, ident_f32[:])
        ident_bf16 = keep.tile([P, P], BF16)
        make_identity(nc, ident_bf16[:])
        b1_rows = keep.tile([P, P], BF16)
        nc.vector.memset(b1_rows[:], 0.0)
        row_0 = keep.tile([P, P], BF16)
        nc.vector.memset(row_0[:], 0.0)
        nc.vector.memset(row_0[0:1, :], 1.0)
        b2_rows = keep.tile([P, D], BF16)
        nc.vector.memset(b2_rows[:], 0.0)

        raw = {}

        def w2_piece(b, piece):
            return divmod(2 * (b - F_BLOCKS) + piece, F_BLOCKS)

        def load_piece(b, piece):
            if piece == 0:
                raw[b] = raw_pool.tile([P, 2, PACK, K_PASS], BF16, name="raw")
            if b < F_BLOCKS:
                source = W1[
                    piece * K_PASS : (piece + 1) * K_PASS, b * K_PASS : (b + 1) * K_PASS
                ].rearrange("(p j) x -> p j x", j=PACK)
            else:
                n, g = w2_piece(b, piece)
                source = W2[
                    g * K_PASS : (g + 1) * K_PASS, n * N_TILE : (n + 1) * N_TILE
                ].rearrange("(j p) x -> p j x", p=P)
            nc.sync.dma_start(out=raw[b][:, piece], in_=source)

        def load_block(b):
            load_piece(b, 0)
            load_piece(b, 1)

        h_sb = keep.tile([P, TOK_TILES, D], BF16)
        h_view = h_rows.rearrange("(m p) d -> p m d", p=P)

        def load_h(pair):
            tiles = slice(2 * pair, 2 * pair + 2)
            nc.sync.dma_start(out=h_sb[:, tiles, :], in_=h_view[:, tiles, :])

        load_piece(0, 0)
        load_piece(0, 1)
        load_h(0)
        nc.sync.dma_start(out=b2_rows[0:1, :], in_=b2.rearrange("(o d) -> o d", o=1))
        load_piece(1, 0)
        load_h(1)
        load_piece(1, 1)
        nc.sync.dma_start(out=b1_rows[0 : F // P, :], in_=b1.rearrange("(i p) -> i p", p=P))
        for b in range(2, AHEAD):
            load_block(b)
        g2_all = keep.tile([P, D], BF16)
        nc.sync.dma_start(out=g2_all[:], in_=g2.partition_broadcast(P))
        beta2_all = keep.tile([P, D], BF16)
        nc.sync.dma_start(out=beta2_all[:], in_=beta2.partition_broadcast(P))

        grouped = {}
        packed = {}

        def new_grouped(b):
            for piece in range(2):
                grouped[(b, piece)] = grouped_pool.tile(
                    [P, K_PASS, PACK], BF16, name="grouped", align_bytes=64
                )

        def regroup_piece(b, piece, split, end=K_PASS):
            for engine_copy, first, last in (
                (nc.vector.tensor_copy, 0, split), (nc.scalar.copy, split, end)
            ):
                if first < last:
                    regroup(
                        engine_copy, grouped[(b, piece)][:, first:last, :],
                        raw[b][:, piece, :, first:last],
                    )

        def regroup_block(b):
            new_grouped(b)
            if b < F_BLOCKS:
                splits = (K_PASS, VECTOR_EXTRA_COLS)
            else:
                splits = (K_PASS - SCALAR_EXTRA_COLS, 0)
            if b in moved:
                regroup_piece(b, 0, K_PASS)
                regroup_piece(b, 1, VECTOR_EXTRA_COLS, K_PASS - MOVED_COLS)
                return
            for piece in range(2):
                regroup_piece(b, piece, splits[piece])

        def take_moved(b):
            nc.scalar.copy(
                out=grouped[(b, 1)][:, K_PASS - MOVED_COLS :, :], in_=moved[b][:]
            )

        moved = {}

        def move_columns(b):
            moved[b] = psum.tile([P, MOVED_COLS, PACK], BF16, name="moved", tag="bank")
            for k in range(0, MOVED_COLS, P):
                first = K_PASS - MOVED_COLS + k
                nc.tensor.matmul(
                    out=moved[b][:, k : k + P, :].rearrange("p w j -> p j w"),
                    lhsT=ident_bf16[:], rhs=raw[b][:, 1, :, first : first + P],
                    start=True, stop=True,
                )

        def quantise_piece(b, piece):
            codes = codes_pool.tile([P, K_PASS], U32, name="codes", align_bytes=64)
            scales = codes_pool.tile([P, K_PASS], U8, name="scales", align_bytes=64)
            nc.vector.quantize_mx(
                out=codes[:].bitcast(FP8X4),
                scales=scales[:],
                in_=grouped[(b, piece)][:].rearrange("p w j -> p (w j)"),
            )
            packed[(b, piece)] = (codes, scales)

        h_grouped = keep.tile([P, D_PASSES, TOK * PACK], BF16, align_bytes=64)
        h_codes = keep.tile([P, D_PASSES, TOK], U32, align_bytes=64)
        h_scales = keep.tile([P, D_PASSES, TOK], U8, align_bytes=64)
        b1_cols = keep.tile([P, F // P], F32)
        hid_codes = keep.tile([P, F_BLOCKS, TOK], U32, align_bytes=64)
        hid_scales = keep.tile([P, F_BLOCKS, TOK], U8, align_bytes=64)
        hid_acc = {}
        hid_bf = {}
        hid_grouped = {}
        out_acc = {}

        def first_matmul(g):
            hid_acc[g] = []
            for j in range(PACK):
                cols = slice(j * P, (j + 1) * P)
                acc = psum.tile([P, TOK], F32, name="acc", tag="bank")
                for c in range(D_PASSES):
                    codes, scales = packed[(g, c)]
                    nc.tensor.matmul_mx(
                        out=acc[:],
                        lhsT=codes[:, cols].bitcast(FP8X4),
                        lhsT_scale=scales[:, cols],
                        rhs=h_codes[:, c, :].bitcast(FP8X4),
                        rhs_scale=h_scales[:, c, :],
                        start=(c == 0),
                        stop=(c == D_PASSES - 1),
                    )
                hid_acc[g].append(acc)

        def relu_block(g):
            hid_bf[g] = hid_pool.tile([P, PACK, TOK], BF16, name="hid_bf")
            for j in range(PACK):
                i = g * PACK + j
                nc.scalar.activation(
                    out=hid_bf[g][:, j, :], in_=hid_acc[g][j][:], func=ACT.Relu,
                    bias=b1_cols[:, i : i + 1], scale=1.0,
                )

        def regroup_hid(g):
            hid_grouped[g] = grouped_pool.tile(
                [P, TOK, PACK], BF16, name="grouped", align_bytes=64
            )
            regroup(nc.vector.tensor_copy, hid_grouped[g][:], hid_bf[g][:])

        def quantise_hid(g):
            nc.vector.quantize_mx(
                out=hid_codes[:, g, :].bitcast(FP8X4),
                scales=hid_scales[:, g, :],
                in_=hid_grouped[g][:].rearrange("p w j -> p (w j)"),
            )

        def second_matmul(b, piece):
            n, g = w2_piece(b, piece)
            codes, scales = packed[(b, piece)]
            for m in range(TOK_TILES):
                if g == 0:
                    out_acc[(m, n)] = psum.tile([P, N_TILE], F32, name="out_acc", tag="bank")
                toks = slice(m * P, (m + 1) * P)
                nc.tensor.matmul_mx(
                    out=out_acc[(m, n)][:],
                    lhsT=hid_codes[:, g, toks].bitcast(FP8X4),
                    lhsT_scale=hid_scales[:, g, toks],
                    rhs=codes[:].bitcast(FP8X4),
                    rhs_scale=scales[:],
                    start=(g == 0),
                    stop=(g == F_BLOCKS - 1),
                )

        def regroup_h(pair):
            words_per_pass = K_PASS // 2
            for c in range(D_PASSES):
                xt = psum.tile([P, 2, 2, P], F32, name="xt", tag="bank")
                for mm in range(2):
                    h_words = h_sb[:, 2 * pair + mm, :].bitcast(F32)
                    for u in range(2):
                        nc.tensor.transpose(
                            xt[:, mm, u, :],
                            h_words[:, c * words_per_pass + u : (c + 1) * words_per_pass : 2],
                            ident_f32[:],
                        )
                dst = (
                    h_grouped[:, c, pair * 2 * P * PACK : (pair + 1) * 2 * P * PACK]
                    .bitcast(F32)
                    .rearrange("p (m k u) -> p m k u", m=2, u=2)
                )
                src = xt[:].rearrange("p m u k -> p m k u")
                if c == 0:
                    nc.vector.tensor_copy(out=dst, in_=src)
                else:
                    nc.scalar.copy(out=dst, in_=src)

        def quantise_h():
            for c in range(D_PASSES):
                nc.vector.quantize_mx(
                    out=h_codes[:, c, :].bitcast(FP8X4),
                    scales=h_scales[:, c, :],
                    in_=h_grouped[:, c, :],
                )

        def spread_b1():
            b1_t = psum.tile([P, P], BF16, name="b1_t", tag="bank")
            nc.tensor.transpose(b1_t[:], b1_rows[:], ident_bf16[:])
            nc.vector.tensor_copy(out=b1_cols[:], in_=b1_t[:, 0 : F // P])

        hb = keep.tile([P, TOK_TILES, D], F32)
        hb_acc = {}

        def residual_matmul(m, n):
            half = slice(n * N_TILE, (n + 1) * N_TILE)
            hb_acc[(m, n)] = psum.tile([P, N_TILE], F32, name="hb_acc", tag="bank")
            nc.tensor.matmul(
                out=hb_acc[(m, n)][:], lhsT=ident_bf16[:], rhs=h_sb[:, m, half],
                start=True, stop=False,
            )
            nc.tensor.matmul(
                out=hb_acc[(m, n)][:], lhsT=row_0[:], rhs=b2_rows[:, half],
                start=False, stop=True,
            )

        def residual_copy(m, n):
            half = slice(n * N_TILE, (n + 1) * N_TILE)
            nc.scalar.copy(out=hb[:, m, half], in_=hb_acc[(m, n)][:])

        r = {}
        r_sum = {}
        neg_mean = {}
        std = {}

        def add_residual(m, n):
            if n == 0:
                r[m] = norm_pool.tile([P, D], F32, name="r")
                r_sum[m] = norm_pool.tile([P, D_HALVES], F32, name="r_sum")
            half = slice(n * N_TILE, (n + 1) * N_TILE)
            nc.vector.scalar_tensor_tensor(
                out=r[m][:, half], in0=out_acc[(m, n)][:], scalar=1.0, in1=hb[:, m, half],
                op0=ALU.mult, op1=ALU.add, accum_out=r_sum[m][:, n : n + 1],
            )

        shift = {}
        half_shift = {}
        sq_sum = {}
        var_0 = {}

        def sum_squares(m, n):
            if n == 0:
                shift[m] = norm_pool.tile([P, 1], F32, name="shift")
                half_shift[m] = norm_pool.tile([P, 1], F32, name="half_shift")
                for column, factor in ((shift[m], -1.0 / N_TILE), (half_shift[m], -1.0 / D)):
                    nc.scalar.activation(
                        out=column[:], in_=r_sum[m][:, 0:1], func=ACT.Copy, scale=factor
                    )
                sq_sum[m] = norm_pool.tile([P, D_HALVES], F32, name="sq_sum")
            half = slice(n * N_TILE, (n + 1) * N_TILE)
            squares = norm_pool.tile([P, N_TILE], BF16, name="squares", bufs=2)
            nc.scalar.activation(
                out=squares[:], in_=r[m][:, half], func=ACT.Square, bias=shift[m][:], scale=1.0,
                accum_out=sq_sum[m][:, n : n + 1],
            )

        new_grouped(0)
        new_grouped(1)
        regroup_piece(0, 0, VECTOR_COLS_START)
        regroup_piece(0, 1, VECTOR_COLS_START)
        quantise_piece(0, 0)
        regroup_h(0)
        for n in range(D_HALVES):
            residual_matmul(0, n)
        quantise_piece(0, 1)
        for n in range(D_HALVES):
            residual_copy(0, n)
        regroup_piece(1, 0, VECTOR_COLS_START)
        regroup_h(1)
        spread_b1()
        for n in range(D_HALVES):
            residual_matmul(1, n)
        quantise_h()
        regroup_piece(1, 1, VECTOR_COLS_START)
        for n in range(D_HALVES):
            residual_copy(1, n)
        quantise_piece(1, 0)
        load_block(AHEAD)
        first_matmul(0)
        move_columns(2)
        later = [(m, n) for m in (2, 3) for n in range(D_HALVES)]
        residual_matmul(*later[0])
        for s in range(2, W_BLOCKS):
            regroup_block(s)
            if s + AHEAD - 1 < W_BLOCKS:
                load_block(s + AHEAD - 1)
            quantise_piece(s - 1, 1)
            if 0 <= s - 3 < F_BLOCKS:
                regroup_hid(s - 3)
            quantise_piece(s, 0)
            if 0 <= s - 2 < F_BLOCKS:
                relu_block(s - 2)
            if s in moved:
                take_moved(s)
            if s - 2 < len(later):
                residual_copy(*later[s - 2])
            if s + 1 < F_BLOCKS:
                move_columns(s + 1)
            if 0 <= s - 1 < F_BLOCKS:
                first_matmul(s - 1)
            if s - 1 < len(later):
                residual_matmul(*later[s - 1])
            if s - 1 >= F_BLOCKS:
                second_matmul(s - 1, 1)
            if s >= F_BLOCKS:
                second_matmul(s, 0)
            if 0 <= s - 3 < F_BLOCKS:
                quantise_hid(s - 3)
            for m in HALF_0_ADDS.get(s, ()):
                add_residual(m, 0)
            if s == W_BLOCKS - 1:
                sum_squares(0, 0)
                sum_squares(1, 0)

        quantise_piece(W_BLOCKS - 1, 1)
        second_matmul(W_BLOCKS - 1, 1)

        def mean(m):
            neg_mean[m] = norm_pool.tile([P, 1], F32, name="neg_mean")
            nc.vector.tensor_scalar(
                out=neg_mean[m][:], in0=r_sum[m][:, 0:1], scalar1=r_sum[m][:, 1:2],
                scalar2=-1.0 / D, op0=ALU.add, op1=ALU.mult,
            )

        def deviation(m):
            gap_sq = norm_pool.tile([P, 1], F32, name="gap_sq")
            nc.scalar.activation(
                out=gap_sq[:], in_=r_sum[m][:, 1:2], func=ACT.Square, bias=half_shift[m][:],
                scale=1.0 / D,
            )
            var_0[m] = norm_pool.tile([P, 1], F32, name="var_0")
            nc.scalar.activation(
                out=var_0[m][:], in_=sq_sum[m][:, 0:1], func=ACT.Identity, bias=eps_col[:],
                scale=1.0 / D,
            )
            sum_squares(m, 1)
            offset = norm_pool.tile([P, 1], F32, name="offset")
            nc.scalar.activation(
                out=offset[:], in_=gap_sq[:], func=ACT.Identity, bias=var_0[m][:], scale=-1.0
            )
            std[m] = norm_pool.tile([P, 1], F32, name="std")
            nc.scalar.activation(
                out=std[m][:], in_=sq_sum[m][:, 1:2], func=ACT.Sqrt, bias=offset[:],
                scale=1.0 / D,
            )

        norm_rows = {}

        def spread_row(name, rows):
            norm_rows[name] = []
            for n in range(D_HALVES):
                bank = psum.tile([P, N_TILE], F32, name=name, tag="bank")
                nc.tensor.matmul(
                    out=bank[:], lhsT=row_0[:], rhs=rows[:, n * N_TILE : (n + 1) * N_TILE],
                    start=True, stop=True,
                )
                norm_rows[name].append(bank)

        def store(queue, m, n, y):
            half = slice(n * N_TILE, (n + 1) * N_TILE)
            queue.dma_start(out=out_rows[m * P : (m + 1) * P, half], in_=y[:, half])

        y = {}
        rstd = {}

        def weigh(m, n):
            if n == 0:
                y[m] = norm_pool.tile([P, D], F32, name="y")
            half = slice(n * N_TILE, (n + 1) * N_TILE)
            nc.vector.scalar_tensor_tensor(
                out=y[m][:, half], in0=r[m][:, half], scalar=neg_mean[m][:],
                in1=norm_rows["g2_psum"][n][:], op0=ALU.add, op1=ALU.mult,
            )

        def invert(m):
            rstd[m] = norm_pool.tile([P, 1], F32, name="rstd")
            nc.vector.reciprocal(out=rstd[m][:], in_=std[m][:])

        def finish_by_vector(m, n):
            half = slice(n * N_TILE, (n + 1) * N_TILE)
            nc.vector.scalar_tensor_tensor(
                out=y[m][:, half], in0=y[m][:, half], scalar=rstd[m][:],
                in1=norm_rows["beta2_psum"][n][:], op0=ALU.mult, op1=ALU.add,
            )
            store(nc.sync, m, n, y[m])

        def normalise_without_vector(m):
            z_bias = norm_pool.tile([P, 1], F32, name="z_bias", bufs=1)
            nc.vector.tensor_scalar(
                out=z_bias[:], in0=neg_mean[m][:], scalar1=rstd[m][:], scalar2=None, op0=ALU.mult
            )
            z = norm_pool.tile([P, D], F32, name="y")
            for n in range(D_HALVES):
                half = slice(n * N_TILE, (n + 1) * N_TILE)
                nc.scalar.activation(
                    out=z[:, half], in_=r[m][:, half], func=ACT.Identity, bias=z_bias[:],
                    scale=rstd[m][:],
                )
                for op, rows in ((ALU.mult, g2_all), (ALU.add, beta2_all)):
                    nc.gpsimd.tensor_tensor(
                        out=z[:, half], in0=z[:, half], in1=rows[:, half], op=op
                    )
            return z

        for m in range(2, TOK_TILES - 1):
            sum_squares(m, 0)
        add_residual(3, 0)
        sum_squares(3, 0)
        spread_row("g2_psum", g2_all)
        spread_row("beta2_psum", beta2_all)
        for m in range(TOK_TILES):
            add_residual(m, 1)
            if m >= 1:
                mean(m - 1)
            if m < 2:
                deviation(m)
        invert(0)
        mean(3)
        z = normalise_without_vector(0)
        weigh(1, 0)
        invert(1)
        weigh(1, 1)
        deviation(2)
        deviation(3)
        finish_by_vector(1, 0)
        finish_by_vector(1, 1)
        weigh(2, 0)
        weigh(2, 1)
        invert(2)
        weigh(3, 0)
        weigh(3, 1)
        invert(3)
        finish_by_vector(2, 0)
        finish_by_vector(2, 1)
        store(nc.scalar, 0, 0, z)
        finish_by_vector(3, 0)
        finish_by_vector(3, 1)
        store(nc.scalar, 0, 1, z)
